import numpy as np
import ml_dtypes


def mxq(x, axis, fmt="e4m3"):
    dtype, down = {"e4m3": (ml_dtypes.float8_e4m3fn, 7), "e5m2": (ml_dtypes.float8_e5m2, 14)}[fmt]
    v = np.moveaxis(np.asarray(x, np.float32).astype(ml_dtypes.bfloat16).astype(np.float64), axis, -1)
    blocks = v.reshape(v.shape[:-1] + (-1, 32))
    amax = np.abs(blocks).max(-1, keepdims=True)
    byte = np.maximum(np.where(amax > 0, np.frexp(amax)[1] - 1 + 127, 0) - down, 1)
    scale = np.exp2(byte - 127.0)
    codes = (blocks / scale).astype(np.float32).astype(dtype).astype(np.float64)
    return np.moveaxis((codes * scale).reshape(v.shape), -1, axis)


WIDE = False


def mx_kscale(k):
    if not WIDE:
        return np.ones(k)
    levels = np.array([20, -20, 10, -10, 0])
    a = np.random.permutation(np.resize(levels, k // 512 * 4)).reshape(k // 512, 4)
    idx = np.arange(k)
    return np.exp2(a[idx // 512, idx % 128 // 32])


BF16 = ml_dtypes.bfloat16


def bf(x):
    return np.asarray(x, np.float32).astype(BF16)


def f64(x):
    return np.asarray(x).astype(np.float64)


B, Nb1, Nw1, Nb2x, Nb2y, Nw2x, Nw2y, R, C = 1024, 2, 16, 4, 2, 16, 16, 128, 2
J1 = Nb1 * Nb1
K1 = C * Nw1 * Nw1
J3 = Nb2x * Nb2y
L1 = J3 * R
J2 = J3 * J1


def setup_inputs():
    s = mx_kscale(B)
    x = np.random.standard_normal((B, Nb1, Nw1, Nb1, Nw1, C)) * s[:, None, None, None, None, None]
    k1 = np.random.standard_normal((J1, K1, L1)) / np.sqrt(K1)
    b1 = np.random.standard_normal((1, J1, L1)) * 0.3
    g = np.random.standard_normal((B, J2, R)) * np.exp2(np.random.randint(-12, 1, (B, 1, 1))) / s[:, None, None]
    return {"x": bf(x.reshape(B, Nb1 * Nw1 * Nb1 * Nw1, C)),
            "k1": bf(k1),
            "b1": bf(b1),
            "grad_out": bf(g)}


def reference(x, k1, b1, grad_out):
    h = f64(x).reshape(B, Nb1, Nw1, Nb1, Nw1, C).transpose(0, 1, 3, 2, 4, 5).reshape(B, J1, K1)
    gy = f64(grad_out).reshape(B, R, J1, J3).transpose(0, 2, 3, 1).reshape(B, J1, L1)
    hq = mxq(h, 0, "e4m3").transpose(1, 2, 0)
    gq = mxq(gy, 0, "e5m2").transpose(1, 0, 2)
    return hq @ gq

@@ -1,0 +1,136 @@
+from contextlib import ExitStack
+
+import concourse.mybir as mybir
+
+BF16 = mybir.dt.bfloat16
+F32 = mybir.dt.float32
+U32 = mybir.dt.uint32
+U8 = mybir.dt.uint8
+E4M3X4 = mybir.dt.float8_e4m3fn_x4
+E5M2X4 = mybir.dt.float8_e5m2_x4
+
+P = 128
+PACK = 4
+K_PASS = P * PACK
+PASSES = 2
+HALVES = 2
+
+X_HALF = 1024
+G_HALF = 2048
+RUN = 8
+R_HALF = 64
+M = 8
+N_TILE = R_HALF * M
+K_TILE = 128
+K_TILES = 4
+UNIT = N_TILE * PACK
+
+FLOPS = 2 * 4 * 512 * 1024 * 1024
+BYTES = 2 * 1024 * 2048 + 2 * 1024 * 4096 + 4 * 4 * 512 * 1024
+
+
+def load_rows(nc, pool, rows, c, first, width, name):
+    raw = pool.tile([P, PACK, width], BF16, name=name)
+    nc.sync.dma_start(
+        out=raw[:],
+        in_=rows[c * K_PASS : (c + 1) * K_PASS, first : first + width].rearrange(
+            "(p t) f -> p t f", t=PACK
+        ),
+    )
+    return raw
+
+
+def regroup_h(copy, raw, bc, grouped_unit):
+    src = raw[:].rearrange("p t (w b g i) -> p b g w t i", b=HALVES, g=4, i=RUN)
+    dst = grouped_unit.rearrange("p (w g i t) -> p g w t i", g=4, i=RUN, t=PACK)
+    for g in range(4):
+        copy(out=dst[:, g], in_=src[:, bc, g])
+
+
+def regroup_gy(copy, raw, j, grouped_unit):
+    src = raw[:].rearrange("p t (r j m) -> p j r t m", j=4, m=M)
+    dst = grouped_unit.rearrange("p (r m t) -> p r t m", m=M, t=PACK)
+    copy(out=dst, in_=src[:, j])
+
+
+def tile_switchnet_fstar_pa_kernel(tc, x, k1, b1, grad_out, out):
+    nc = tc.nc
+    x_rows = x.rearrange("b g c -> b (g c)")
+    g_rows = grad_out.rearrange("b s r -> b (s r)")
+
+    with ExitStack() as ctx:
+        raw_pool = ctx.enter_context(tc.tile_pool(name="raw", bufs=1))
+        stage = ctx.enter_context(tc.tile_pool(name="stage", bufs=3))
+        keep = ctx.enter_context(tc.tile_pool(name="keep", bufs=1))
+        results = ctx.enter_context(tc.tile_pool(name="results", bufs=4))
+        psum = ctx.enter_context(tc.psum_pool(name="psum", bufs=8))
+
+        raw_x = {}
+        raw_g = {}
+        for c in range(PASSES):
+            raw_x[c, 0] = load_rows(nc, raw_pool, x_rows, c, 0, X_HALF, "raw_x%d0" % c)
+        for c in range(PASSES):
+            for rh in range(HALVES):
+                raw_g[c, rh] = load_rows(
+                    nc, raw_pool, g_rows, c, rh * G_HALF, G_HALF, "raw_g%d%d" % (c, rh)
+                )
+        for c in range(PASSES):
+            raw_x[c, 1] = load_rows(nc, raw_pool, x_rows, c, X_HALF, X_HALF, "raw_x%d1" % c)
+
+        def quantise_two_units(regroup, raw, first, fp8x4, name):
+            grouped = stage.tile([P, 2 * UNIT], BF16, align_bytes=64)
+            regroup(nc.vector.tensor_copy, raw, first, grouped[:, 0:UNIT])
+            regroup(nc.scalar.copy, raw, first + 1, grouped[:, UNIT : 2 * UNIT])
+            codes = keep.tile([P, 2 * N_TILE], U32, align_bytes=64, name="codes_" + name)
+            scales = keep.tile([P, 2 * N_TILE], U8, align_bytes=64, name="scales_" + name)
+            nc.vector.quantize_mx(out=codes[:].bitcast(fp8x4), scales=scales[:], in_=grouped[:])
+            return codes, scales
+
+        h_mx = {}
+        g_mx = {}
+        for c in range(PASSES):
+            h_mx[c, 0] = quantise_two_units(regroup_h, raw_x[c, 0], 0, E4M3X4, "h%d0" % c)
+        for c in range(PASSES):
+            for rh in range(HALVES):
+                for br in range(HALVES):
+                    g_mx[c, rh, br] = quantise_two_units(
+                        regroup_gy, raw_g[c, rh], 2 * br, E5M2X4, "g%d%d%d" % (c, rh, br)
+                    )
+        for c in range(PASSES):
+            h_mx[c, 1] = quantise_two_units(regroup_h, raw_x[c, 1], 0, E4M3X4, "h%d1" % c)
+
+        for br in range(HALVES):
+            for bc in range(HALVES):
+                acc = {}
+                for c in range(PASSES):
+                    h_codes, h_scales = h_mx[c, br]
+                    for kt in range(K_TILES):
+                        k_cols = slice(bc * N_TILE + kt * K_TILE, bc * N_TILE + (kt + 1) * K_TILE)
+                        for rh in range(HALVES):
+                            g_codes, g_scales = g_mx[c, rh, br]
+                            n_cols = slice(bc * N_TILE, (bc + 1) * N_TILE)
+                            if c == 0:
+                                acc[kt, rh] = psum.tile([P, N_TILE], F32, name="acc")
+                            nc.tensor.matmul_mx(
+                                out=acc[kt, rh][:],
+                                lhsT=h_codes[:, k_cols].bitcast(E4M3X4),
+                                lhsT_scale=h_scales[:, k_cols],
+                                rhs=g_codes[:, n_cols].bitcast(E5M2X4),
+                                rhs_scale=g_scales[:, n_cols],
+                                start=(c == 0),
+                                stop=(c == PASSES - 1),
+                            )
+                for kt in range(K_TILES):
+                    rows_out = results.tile([P, M, HALVES, R_HALF], F32)
+                    nc.vector.tensor_copy(
+                        out=rows_out[:, :, 0, :],
+                        in_=acc[kt, 0][:].rearrange("p (r m) -> p m r", m=M),
+                    )
+                    nc.scalar.copy(
+                        out=rows_out[:, :, 1, :],
+                        in_=acc[kt, 1][:].rearrange("p (r m) -> p m r", m=M),
+                    )
+                    nc.sync.dma_start(
+                        out=out[2 * br + bc, kt * K_TILE : (kt + 1) * K_TILE, :],
+                        in_=rows_out[:].rearrange("p m h r -> p (m h r)"),
+                    )

@@ -13,11 +13,13 @@ P = 128
 PACK = 4
 K_PASS = P * PACK
 PASSES = 2
+BLOCKS = 4
 HALVES = 2
 
 X_HALF = 1024
 G_HALF = 2048
 RUN = 8
+RUNS = 4
 R_HALF = 64
 M = 8
 N_TILE = R_HALF * M
@@ -29,108 +31,134 @@ FLOPS = 2 * 4 * 512 * 1024 * 1024
 BYTES = 2 * 1024 * 2048 + 2 * 1024 * 4096 + 4 * 4 * 512 * 1024
 
 
-def load_rows(nc, pool, rows, c, first, width, name):
-    raw = pool.tile([P, PACK, width], BF16, name=name)
-    nc.sync.dma_start(
-        out=raw[:],
-        in_=rows[c * K_PASS : (c + 1) * K_PASS, first : first + width].rearrange(
-            "(p t) f -> p t f", t=PACK
-        ),
-    )
-    return raw
-
-
-def regroup_h(copy, raw, bc, grouped_unit):
-    src = raw[:].rearrange("p t (w b g i) -> p b g w t i", b=HALVES, g=4, i=RUN)
-    dst = grouped_unit.rearrange("p (w g i t) -> p g w t i", g=4, i=RUN, t=PACK)
-    for g in range(4):
-        copy(out=dst[:, g], in_=src[:, bc, g])
-
-
-def regroup_gy(copy, raw, j, grouped_unit):
-    src = raw[:].rearrange("p t (r j m) -> p j r t m", j=4, m=M)
-    dst = grouped_unit.rearrange("p (r m t) -> p r t m", m=M, t=PACK)
-    copy(out=dst, in_=src[:, j])
-
-
 def tile_switchnet_fstar_pa_kernel(tc, x, k1, b1, grad_out, out):
     nc = tc.nc
     x_rows = x.rearrange("b g c -> b (g c)")
     g_rows = grad_out.rearrange("b s r -> b (s r)")
 
     with ExitStack() as ctx:
+        ctx.enter_context(tc.manual_schedule())
         raw_pool = ctx.enter_context(tc.tile_pool(name="raw", bufs=1))
-        stage = ctx.enter_context(tc.tile_pool(name="stage", bufs=3))
+        stage = ctx.enter_context(tc.tile_pool(name="stage", bufs=4))
         keep = ctx.enter_context(tc.tile_pool(name="keep", bufs=1))
-        results = ctx.enter_context(tc.tile_pool(name="results", bufs=4))
+        results = ctx.enter_context(tc.tile_pool(name="results", bufs=6))
         psum = ctx.enter_context(tc.psum_pool(name="psum", bufs=8))
+
+        def load_rows(rows, c, first, width, name):
+            raw = raw_pool.tile([P, PACK, width], BF16, name=name)
+            nc.sync.dma_start(
+                out=raw[:],
+                in_=rows[c * K_PASS : (c + 1) * K_PASS, first : first + width].rearrange(
+                    "(p t) f -> p t f", t=PACK
+                ),
+            )
+            return raw
 
         raw_x = {}
         raw_g = {}
         for c in range(PASSES):
-            raw_x[c, 0] = load_rows(nc, raw_pool, x_rows, c, 0, X_HALF, "raw_x%d0" % c)
+            raw_x[c, 0] = load_rows(x_rows, c, 0, X_HALF, "raw_x%d0" % c)
         for c in range(PASSES):
             for rh in range(HALVES):
-                raw_g[c, rh] = load_rows(
-                    nc, raw_pool, g_rows, c, rh * G_HALF, G_HALF, "raw_g%d%d" % (c, rh)
-                )
+                raw_g[c, rh] = load_rows(g_rows, c, rh * G_HALF, G_HALF, "raw_g%d%d" % (c, rh))
         for c in range(PASSES):
-            raw_x[c, 1] = load_rows(nc, raw_pool, x_rows, c, X_HALF, X_HALF, "raw_x%d1" % c)
+            raw_x[c, 1] = load_rows(x_rows, c, X_HALF, X_HALF, "raw_x%d1" % c)
 
-        def quantise_two_units(regroup, raw, first, fp8x4, name):
-            grouped = stage.tile([P, 2 * UNIT], BF16, align_bytes=64)
-            regroup(nc.vector.tensor_copy, raw, first, grouped[:, 0:UNIT])
-            regroup(nc.scalar.copy, raw, first + 1, grouped[:, UNIT : 2 * UNIT])
-            codes = keep.tile([P, 2 * N_TILE], U32, align_bytes=64, name="codes_" + name)
-            scales = keep.tile([P, 2 * N_TILE], U8, align_bytes=64, name="scales_" + name)
+        copied = []
+
+        def quantise_copied():
+            grouped, codes, scales, fp8x4 = copied.pop()
             nc.vector.quantize_mx(out=codes[:].bitcast(fp8x4), scales=scales[:], in_=grouped[:])
-            return codes, scales
+
+        def new_unit(fp8x4, name):
+            grouped = stage.tile([P, UNIT], BF16, align_bytes=64, name="grouped")
+            codes = keep.tile([P, N_TILE], U32, align_bytes=64, name="codes_" + name)
+            scales = keep.tile([P, N_TILE], U8, align_bytes=64, name="scales_" + name)
+            return grouped, codes, scales, fp8x4
+
+        def prepare_h(c, j):
+            unit = new_unit(E4M3X4, "h%d%d" % (c, j))
+            src = raw_x[c, j // 2][:].rearrange(
+                "p t (w b g i) -> p b g w t i", b=HALVES, g=RUNS, i=RUN
+            )
+            dst = unit[0][:].rearrange("p (w g i t) -> p g w t i", g=RUNS, i=RUN, t=PACK)
+            for g in range(RUNS // 2):
+                nc.vector.tensor_copy(out=dst[:, g], in_=src[:, j % 2, g])
+            for g in range(RUNS // 2, RUNS):
+                nc.scalar.copy(out=dst[:, g], in_=src[:, j % 2, g])
+            if copied:
+                quantise_copied()
+            copied.append(unit)
+            return unit[1], unit[2]
+
+        def prepare_gy(c, rh, j):
+            unit = new_unit(E5M2X4, "g%d%d%d" % (c, rh, j))
+            src = raw_g[c, rh][:].rearrange("p t (r j m) -> p j r t m", j=BLOCKS, m=M)
+            dst = unit[0][:].rearrange("p (r m t) -> p r t m", m=M, t=PACK)
+            half = R_HALF // 2
+            nc.vector.tensor_copy(out=dst[:, 0:half], in_=src[:, j, 0:half])
+            nc.scalar.copy(out=dst[:, half:R_HALF], in_=src[:, j, half:R_HALF])
+            if copied:
+                quantise_copied()
+            copied.append(unit)
+            return unit[1], unit[2]
 
         h_mx = {}
         g_mx = {}
+        acc = {}
+
+        def multiply(j):
+            for c in range(PASSES):
+                h_codes, h_scales = h_mx[c, j]
+                for rh in range(HALVES):
+                    g_codes, g_scales = g_mx[c, rh, j]
+                    for kt in range(K_TILES):
+                        k_cols = slice(kt * K_TILE, (kt + 1) * K_TILE)
+                        if c == 0:
+                            acc[j, kt, rh] = psum.tile([P, N_TILE], F32, name="acc")
+                        nc.tensor.matmul_mx(
+                            out=acc[j, kt, rh][:],
+                            lhsT=h_codes[:, k_cols].bitcast(E4M3X4),
+                            lhsT_scale=h_scales[:, k_cols],
+                            rhs=g_codes[:].bitcast(E5M2X4),
+                            rhs_scale=g_scales[:],
+                            start=(c == 0),
+                            stop=(c == PASSES - 1),
+                        )
+
+        def store(j):
+            for kt in range(K_TILES):
+                rows_out = results.tile([P, M, HALVES, R_HALF], F32, name="rows_out")
+                nc.vector.tensor_copy(
+                    out=rows_out[:, :, 0, :],
+                    in_=acc[j, kt, 0][:].rearrange("p (r m) -> p m r", m=M),
+                )
+                nc.scalar.copy(
+                    out=rows_out[:, :, 1, :],
+                    in_=acc[j, kt, 1][:].rearrange("p (r m) -> p m r", m=M),
+                )
+                nc.sync.dma_start(
+                    out=out[j, kt * K_TILE : (kt + 1) * K_TILE, :],
+                    in_=rows_out[:].rearrange("p m h r -> p (m h r)"),
+                )
+
+        last_c, last_rh = PASSES - 1, HALVES - 1
         for c in range(PASSES):
-            h_mx[c, 0] = quantise_two_units(regroup_h, raw_x[c, 0], 0, E4M3X4, "h%d0" % c)
+            for j in range(HALVES):
+                h_mx[c, j] = prepare_h(c, j)
         for c in range(PASSES):
             for rh in range(HALVES):
-                for br in range(HALVES):
-                    g_mx[c, rh, br] = quantise_two_units(
-                        regroup_gy, raw_g[c, rh], 2 * br, E5M2X4, "g%d%d%d" % (c, rh, br)
-                    )
-        for c in range(PASSES):
-            h_mx[c, 1] = quantise_two_units(regroup_h, raw_x[c, 1], 0, E4M3X4, "h%d1" % c)
+                if (c, rh) != (last_c, last_rh):
+                    for j in range(BLOCKS):
+                        g_mx[c, rh, j] = prepare_gy(c, rh, j)
 
-        for br in range(HALVES):
-            for bc in range(HALVES):
-                acc = {}
+        for j in range(BLOCKS):
+            if j >= HALVES:
                 for c in range(PASSES):
-                    h_codes, h_scales = h_mx[c, br]
-                    for kt in range(K_TILES):
-                        k_cols = slice(bc * N_TILE + kt * K_TILE, bc * N_TILE + (kt + 1) * K_TILE)
-                        for rh in range(HALVES):
-                            g_codes, g_scales = g_mx[c, rh, br]
-                            n_cols = slice(bc * N_TILE, (bc + 1) * N_TILE)
-                            if c == 0:
-                                acc[kt, rh] = psum.tile([P, N_TILE], F32, name="acc")
-                            nc.tensor.matmul_mx(
-                                out=acc[kt, rh][:],
-                                lhsT=h_codes[:, k_cols].bitcast(E4M3X4),
-                                lhsT_scale=h_scales[:, k_cols],
-                                rhs=g_codes[:, n_cols].bitcast(E5M2X4),
-                                rhs_scale=g_scales[:, n_cols],
-                                start=(c == 0),
-                                stop=(c == PASSES - 1),
-                            )
-                for kt in range(K_TILES):
-                    rows_out = results.tile([P, M, HALVES, R_HALF], F32)
-                    nc.vector.tensor_copy(
-                        out=rows_out[:, :, 0, :],
-                        in_=acc[kt, 0][:].rearrange("p (r m) -> p m r", m=M),
-                    )
-                    nc.scalar.copy(
-                        out=rows_out[:, :, 1, :],
-                        in_=acc[kt, 1][:].rearrange("p (r m) -> p m r", m=M),
-                    )
-                    nc.sync.dma_start(
-                        out=out[2 * br + bc, kt * K_TILE : (kt + 1) * K_TILE, :],
-                        in_=rows_out[:].rearrange("p m h r -> p (m h r)"),
-                    )
+                    h_mx[c, j] = prepare_h(c, j)
+            g_mx[last_c, last_rh, j] = prepare_gy(last_c, last_rh, j)
+            quantise_copied()
+            if j > 0:
+                store(j - 1)
+            multiply(j)
+        store(BLOCKS - 1)

@@ -76,89 +76,90 @@ def tile_switchnet_fstar_pa_kernel(tc, x, k1, b1, grad_out, out):
             scales = keep.tile([P, N_TILE], U8, align_bytes=64, name="scales_" + name)
             return grouped, codes, scales, fp8x4
 
-        def prepare_h(c, j):
+        def hand_over(unit):
+            if copied:
+                quantise_copied()
+            copied.append(unit)
+            return unit[1], unit[2]
+
+        def prepare_h(c, j, shared):
             unit = new_unit(E4M3X4, "h%d%d" % (c, j))
             src = raw_x[c, j // 2][:].rearrange(
                 "p t (w b g i) -> p b g w t i", b=HALVES, g=RUNS, i=RUN
             )
             dst = unit[0][:].rearrange("p (w g i t) -> p g w t i", g=RUNS, i=RUN, t=PACK)
-            for g in range(RUNS // 2):
-                nc.vector.tensor_copy(out=dst[:, g], in_=src[:, j % 2, g])
-            for g in range(RUNS // 2, RUNS):
-                nc.scalar.copy(out=dst[:, g], in_=src[:, j % 2, g])
-            if copied:
-                quantise_copied()
-            copied.append(unit)
-            return unit[1], unit[2]
+            for g in range(RUNS):
+                if shared and g >= RUNS // 2:
+                    nc.scalar.copy(out=dst[:, g], in_=src[:, j % 2, g])
+                else:
+                    nc.vector.tensor_copy(out=dst[:, g], in_=src[:, j % 2, g])
+            return hand_over(unit)
 
-        def prepare_gy(c, rh, j):
+        def prepare_gy(c, rh, j, shared):
             unit = new_unit(E5M2X4, "g%d%d%d" % (c, rh, j))
             src = raw_g[c, rh][:].rearrange("p t (r j m) -> p j r t m", j=BLOCKS, m=M)
             dst = unit[0][:].rearrange("p (r m t) -> p r t m", m=M, t=PACK)
-            half = R_HALF // 2
-            nc.vector.tensor_copy(out=dst[:, 0:half], in_=src[:, j, 0:half])
-            nc.scalar.copy(out=dst[:, half:R_HALF], in_=src[:, j, half:R_HALF])
-            if copied:
-                quantise_copied()
-            copied.append(unit)
-            return unit[1], unit[2]
+            if shared:
+                half = R_HALF // 2
+                nc.vector.tensor_copy(out=dst[:, 0:half], in_=src[:, j, 0:half])
+                nc.scalar.copy(out=dst[:, half:R_HALF], in_=src[:, j, half:R_HALF])
+            else:
+                nc.vector.tensor_copy(out=dst, in_=src[:, j])
+            return hand_over(unit)
 
         h_mx = {}
         g_mx = {}
         acc = {}
 
-        def multiply(j):
-            for c in range(PASSES):
-                h_codes, h_scales = h_mx[c, j]
-                for rh in range(HALVES):
+        def multiply_tile(j, kt):
+            k_cols = slice(kt * K_TILE, (kt + 1) * K_TILE)
+            for rh in range(HALVES):
+                acc[j, kt, rh] = psum.tile([P, N_TILE], F32, name="acc")
+                for c in range(PASSES):
+                    h_codes, h_scales = h_mx[c, j]
                     g_codes, g_scales = g_mx[c, rh, j]
-                    for kt in range(K_TILES):
-                        k_cols = slice(kt * K_TILE, (kt + 1) * K_TILE)
-                        if c == 0:
-                            acc[j, kt, rh] = psum.tile([P, N_TILE], F32, name="acc")
-                        nc.tensor.matmul_mx(
-                            out=acc[j, kt, rh][:],
-                            lhsT=h_codes[:, k_cols].bitcast(E4M3X4),
-                            lhsT_scale=h_scales[:, k_cols],
-                            rhs=g_codes[:].bitcast(E5M2X4),
-                            rhs_scale=g_scales[:],
-                            start=(c == 0),
-                            stop=(c == PASSES - 1),
-                        )
+                    nc.tensor.matmul_mx(
+                        out=acc[j, kt, rh][:],
+                        lhsT=h_codes[:, k_cols].bitcast(E4M3X4),
+                        lhsT_scale=h_scales[:, k_cols],
+                        rhs=g_codes[:].bitcast(E5M2X4),
+                        rhs_scale=g_scales[:],
+                        start=(c == 0),
+                        stop=(c == PASSES - 1),
+                    )
 
-        def store(j):
-            for kt in range(K_TILES):
-                rows_out = results.tile([P, M, HALVES, R_HALF], F32, name="rows_out")
-                nc.vector.tensor_copy(
-                    out=rows_out[:, :, 0, :],
-                    in_=acc[j, kt, 0][:].rearrange("p (r m) -> p m r", m=M),
-                )
-                nc.scalar.copy(
-                    out=rows_out[:, :, 1, :],
-                    in_=acc[j, kt, 1][:].rearrange("p (r m) -> p m r", m=M),
-                )
-                nc.sync.dma_start(
-                    out=out[j, kt * K_TILE : (kt + 1) * K_TILE, :],
-                    in_=rows_out[:].rearrange("p m h r -> p (m h r)"),
-                )
+        def store_tile(j, kt, copy_first_bank):
+            rows_out = results.tile([P, M, HALVES, R_HALF], F32, name="rows_out")
+            copy_first_bank(
+                out=rows_out[:, :, 0, :], in_=acc[j, kt, 0][:].rearrange("p (r m) -> p m r", m=M)
+            )
+            nc.scalar.copy(
+                out=rows_out[:, :, 1, :], in_=acc[j, kt, 1][:].rearrange("p (r m) -> p m r", m=M)
+            )
+            nc.sync.dma_start(
+                out=out[j, kt * K_TILE : (kt + 1) * K_TILE, :],
+                in_=rows_out[:].rearrange("p m h r -> p (m h r)"),
+            )
 
         last_c, last_rh = PASSES - 1, HALVES - 1
         for c in range(PASSES):
             for j in range(HALVES):
-                h_mx[c, j] = prepare_h(c, j)
+                h_mx[c, j] = prepare_h(c, j, True)
         for c in range(PASSES):
             for rh in range(HALVES):
                 if (c, rh) != (last_c, last_rh):
                     for j in range(BLOCKS):
-                        g_mx[c, rh, j] = prepare_gy(c, rh, j)
+                        g_mx[c, rh, j] = prepare_gy(c, rh, j, True)
 
         for j in range(BLOCKS):
             if j >= HALVES:
                 for c in range(PASSES):
-                    h_mx[c, j] = prepare_h(c, j)
-            g_mx[last_c, last_rh, j] = prepare_gy(last_c, last_rh, j)
+                    h_mx[c, j] = prepare_h(c, j, False)
+            g_mx[last_c, last_rh, j] = prepare_gy(last_c, last_rh, j, j < HALVES)
             quantise_copied()
-            if j > 0:
-                store(j - 1)
-            multiply(j)
-        store(BLOCKS - 1)
+            for kt in range(K_TILES):
+                if j > 0:
+                    store_tile(j - 1, kt, nc.scalar.copy)
+                multiply_tile(j, kt)
+        for kt in range(K_TILES):
+            store_tile(BLOCKS - 1, kt, nc.vector.tensor_copy)

@@ -42,7 +42,7 @@ def tile_switchnet_fstar_pa_kernel(tc, x, k1, b1, grad_out, out):
         stage = ctx.enter_context(tc.tile_pool(name="stage", bufs=4))
         keep = ctx.enter_context(tc.tile_pool(name="keep", bufs=1))
         results = ctx.enter_context(tc.tile_pool(name="results", bufs=6))
-        psum = ctx.enter_context(tc.psum_pool(name="psum", bufs=8))
+        psum = ctx.enter_context(tc.psum_pool(name="psum", bufs=1))
 
         def load_rows(rows, c, first, width, name):
             raw = raw_pool.tile([P, PACK, width], BF16, name=name)
@@ -111,22 +111,21 @@ def tile_switchnet_fstar_pa_kernel(tc, x, k1, b1, grad_out, out):
         g_mx = {}
         acc = {}
 
-        def multiply_tile(j, kt):
+        def multiply(j, kt, rh, c):
+            if c == 0:
+                acc[j, kt, rh] = psum.tile([P, N_TILE], F32, name="acc%d%d" % (kt, rh))
+            h_codes, h_scales = h_mx[c, j]
+            g_codes, g_scales = g_mx[c, rh, j]
             k_cols = slice(kt * K_TILE, (kt + 1) * K_TILE)
-            for rh in range(HALVES):
-                acc[j, kt, rh] = psum.tile([P, N_TILE], F32, name="acc")
-                for c in range(PASSES):
-                    h_codes, h_scales = h_mx[c, j]
-                    g_codes, g_scales = g_mx[c, rh, j]
-                    nc.tensor.matmul_mx(
-                        out=acc[j, kt, rh][:],
-                        lhsT=h_codes[:, k_cols].bitcast(E4M3X4),
-                        lhsT_scale=h_scales[:, k_cols],
-                        rhs=g_codes[:].bitcast(E5M2X4),
-                        rhs_scale=g_scales[:],
-                        start=(c == 0),
-                        stop=(c == PASSES - 1),
-                    )
+            nc.tensor.matmul_mx(
+                out=acc[j, kt, rh][:],
+                lhsT=h_codes[:, k_cols].bitcast(E4M3X4),
+                lhsT_scale=h_scales[:, k_cols],
+                rhs=g_codes[:].bitcast(E5M2X4),
+                rhs_scale=g_scales[:],
+                start=(c == 0),
+                stop=(c == PASSES - 1),
+            )
 
         def store_tile(j, kt, copy_first_bank):
             rows_out = results.tile([P, M, HALVES, R_HALF], F32, name="rows_out")
@@ -141,25 +140,31 @@ def tile_switchnet_fstar_pa_kernel(tc, x, k1, b1, grad_out, out):
                 in_=rows_out[:].rearrange("p m h r -> p (m h r)"),
             )
 
-        last_c, last_rh = PASSES - 1, HALVES - 1
+        last_piece = (PASSES - 1, HALVES - 1)
         for c in range(PASSES):
             for j in range(HALVES):
                 h_mx[c, j] = prepare_h(c, j, True)
         for c in range(PASSES):
             for rh in range(HALVES):
-                if (c, rh) != (last_c, last_rh):
-                    for j in range(BLOCKS):
-                        g_mx[c, rh, j] = prepare_gy(c, rh, j, True)
+                for j in range(1 if (c, rh) == last_piece else BLOCKS):
+                    g_mx[c, rh, j] = prepare_gy(c, rh, j, True)
+                if (c, rh) == last_piece:
+                    quantise_copied()
+                for kt in range(K_TILES):
+                    multiply(0, kt, rh, c)
 
-        for j in range(BLOCKS):
+        for j in range(1, BLOCKS):
             if j >= HALVES:
                 for c in range(PASSES):
                     h_mx[c, j] = prepare_h(c, j, False)
-            g_mx[last_c, last_rh, j] = prepare_gy(last_c, last_rh, j, j < HALVES)
+            g_mx[last_piece[0], last_piece[1], j] = prepare_gy(
+                last_piece[0], last_piece[1], j, j < HALVES
+            )
             quantise_copied()
             for kt in range(K_TILES):
-                if j > 0:
-                    store_tile(j - 1, kt, nc.scalar.copy)
-                multiply_tile(j, kt)
+                store_tile(j - 1, kt, nc.scalar.copy)
+                for rh in range(HALVES):
+                    for c in range(PASSES):
+                        multiply(j, kt, rh, c)
         for kt in range(K_TILES):
             store_tile(BLOCKS - 1, kt, nc.vector.tensor_copy)

@@ -162,7 +162,8 @@ def tile_switchnet_fstar_pa_kernel(tc, x, k1, b1, grad_out, out):
             )
             quantise_copied()
             for kt in range(K_TILES):
-                store_tile(j - 1, kt, nc.scalar.copy)
+                last_tile = kt == K_TILES - 1
+                store_tile(j - 1, kt, nc.vector.tensor_copy if last_tile else nc.scalar.copy)
                 for rh in range(HALVES):
                     for c in range(PASSES):
                         multiply(j, kt, rh, c)

@@ -45,7 +45,7 @@ def tile_switchnet_fstar_pa_kernel(tc, x, k1, b1, grad_out, out):
         psum = ctx.enter_context(tc.psum_pool(name="psum", bufs=1))
 
         def load_rows(rows, c, first, width, name):
-            raw = raw_pool.tile([P, PACK, width], BF16, name=name)
+            raw = raw_pool.tile([P, PACK, width], BF16, align_bytes=256, name=name)
             nc.sync.dma_start(
                 out=raw[:],
                 in_=rows[c * K_PASS : (c + 1) * K_PASS, first : first + width].rearrange(
@@ -128,7 +128,7 @@ def tile_switchnet_fstar_pa_kernel(tc, x, k1, b1, grad_out, out):
             )
 
         def store_tile(j, kt, copy_first_bank):
-            rows_out = results.tile([P, M, HALVES, R_HALF], F32, name="rows_out")
+            rows_out = results.tile([P, M, HALVES, R_HALF], F32, align_bytes=256, name="rows_out")
             copy_first_bank(
                 out=rows_out[:, :, 0, :], in_=acc[j, kt, 0][:].rearrange("p (r m) -> p m r", m=M)
             )

@@ -27,6 +27,10 @@ K_TILE = 128
 K_TILES = 4
 UNIT = N_TILE * PACK
 
+HELD_BACK = (0, 1)
+RUNS_AHEAD = (1, 0)
+URGENT_VECTOR_SHARE = 40
+
 FLOPS = 2 * 4 * 512 * 1024 * 1024
 BYTES = 2 * 1024 * 2048 + 2 * 1024 * 4096 + 4 * 4 * 512 * 1024
 
@@ -66,9 +70,12 @@ def tile_switchnet_fstar_pa_kernel(tc, x, k1, b1, grad_out, out):
 
         copied = []
 
-        def quantise_copied():
-            grouped, codes, scales, fp8x4 = copied.pop()
+        def quantise(unit):
+            grouped, codes, scales, fp8x4 = unit
             nc.vector.quantize_mx(out=codes[:].bitcast(fp8x4), scales=scales[:], in_=grouped[:])
+
+        def quantise_copied():
+            quantise(copied.pop())
 
         def new_unit(fp8x4, name):
             grouped = stage.tile([P, UNIT], BF16, align_bytes=64, name="grouped")
@@ -97,15 +104,17 @@ def tile_switchnet_fstar_pa_kernel(tc, x, k1, b1, grad_out, out):
 
         def prepare_gy(c, rh, j, shared):
             unit = new_unit(E5M2X4, "g%d%d%d" % (c, rh, j))
+            regroup_gy(unit, c, rh, j, R_HALF // 2 if shared else R_HALF)
+            return hand_over(unit)
+
+        def regroup_gy(unit, c, rh, j, vector_share):
             src = raw_g[c, rh][:].rearrange("p t (r j m) -> p j r t m", j=BLOCKS, m=M)
             dst = unit[0][:].rearrange("p (r m t) -> p r t m", m=M, t=PACK)
-            if shared:
-                half = R_HALF // 2
-                nc.vector.tensor_copy(out=dst[:, 0:half], in_=src[:, j, 0:half])
-                nc.scalar.copy(out=dst[:, half:R_HALF], in_=src[:, j, half:R_HALF])
-            else:
-                nc.vector.tensor_copy(out=dst, in_=src[:, j])
-            return hand_over(unit)
+            nc.vector.tensor_copy(out=dst[:, 0:vector_share], in_=src[:, j, 0:vector_share])
+            if vector_share < R_HALF:
+                nc.scalar.copy(
+                    out=dst[:, vector_share:R_HALF], in_=src[:, j, vector_share:R_HALF]
+                )
 
         h_mx = {}
         g_mx = {}
@@ -146,24 +155,33 @@ def tile_switchnet_fstar_pa_kernel(tc, x, k1, b1, grad_out, out):
                 h_mx[c, j] = prepare_h(c, j, True)
         for c in range(PASSES):
             for rh in range(HALVES):
-                for j in range(1 if (c, rh) == last_piece else BLOCKS):
-                    g_mx[c, rh, j] = prepare_gy(c, rh, j, True)
                 if (c, rh) == last_piece:
-                    quantise_copied()
-                for kt in range(K_TILES):
-                    multiply(0, kt, rh, c)
+                    urgent = new_unit(E5M2X4, "g%d%d0" % (c, rh))
+                    regroup_gy(urgent, c, rh, 0, URGENT_VECTOR_SHARE)
+                    quantise(urgent)
+                    g_mx[c, rh, 0] = urgent[1], urgent[2]
+                else:
+                    for j in range(BLOCKS):
+                        g_mx[c, rh, j] = prepare_gy(c, rh, j, True)
+                if (c, rh) != HELD_BACK:
+                    for kt in range(K_TILES):
+                        multiply(0, kt, rh, c)
+                if (c, rh) == RUNS_AHEAD:
+                    for kt in range(K_TILES):
+                        multiply(0, kt, HELD_BACK[1], HELD_BACK[0])
+        store_tile(0, 0, nc.scalar.copy)
 
         for j in range(1, BLOCKS):
             if j >= HALVES:
                 for c in range(PASSES):
                     h_mx[c, j] = prepare_h(c, j, False)
             g_mx[last_piece[0], last_piece[1], j] = prepare_gy(
-                last_piece[0], last_piece[1], j, j < HALVES
+                last_piece[0], last_piece[1], j, False
             )
             quantise_copied()
             for kt in range(K_TILES):
-                last_tile = kt == K_TILES - 1
-                store_tile(j - 1, kt, nc.vector.tensor_copy if last_tile else nc.scalar.copy)
+                if (j - 1, kt) != (0, 0):
+                    store_tile(j - 1, kt, nc.scalar.copy)
                 for rh in range(HALVES):
                     for c in range(PASSES):
                         multiply(j, kt, rh, c)

@@ -29,6 +29,7 @@ UNIT = N_TILE * PACK
 
 HELD_BACK = (0, 1)
 RUNS_AHEAD = (1, 0)
+IN_TWO_LOADS = ((0, 0), (0, 1), (1, 0))
 URGENT_VECTOR_SHARE = 40
 
 FLOPS = 2 * 4 * 512 * 1024 * 1024
@@ -43,7 +44,7 @@ def tile_switchnet_fstar_pa_kernel(tc, x, k1, b1, grad_out, out):
     with ExitStack() as ctx:
         ctx.enter_context(tc.manual_schedule())
         raw_pool = ctx.enter_context(tc.tile_pool(name="raw", bufs=1))
-        stage = ctx.enter_context(tc.tile_pool(name="stage", bufs=4))
+        stage = ctx.enter_context(tc.tile_pool(name="stage", bufs=8))
         keep = ctx.enter_context(tc.tile_pool(name="keep", bufs=1))
         results = ctx.enter_context(tc.tile_pool(name="results", bufs=6))
         psum = ctx.enter_context(tc.psum_pool(name="psum", bufs=1))
@@ -64,7 +65,12 @@ def tile_switchnet_fstar_pa_kernel(tc, x, k1, b1, grad_out, out):
             raw_x[c, 0] = load_rows(x_rows, c, 0, X_HALF, "raw_x%d0" % c)
         for c in range(PASSES):
             for rh in range(HALVES):
-                raw_g[c, rh] = load_rows(g_rows, c, rh * G_HALF, G_HALF, "raw_g%d%d" % (c, rh))
+                loads = HALVES if (c, rh) in IN_TWO_LOADS else 1
+                width = G_HALF // loads
+                raw_g[c, rh] = [
+                    load_rows(g_rows, c, rh * G_HALF + a * width, width, "raw_g%d%d%d" % (c, rh, a))
+                    for a in range(loads)
+                ]
         for c in range(PASSES):
             raw_x[c, 1] = load_rows(x_rows, c, X_HALF, X_HALF, "raw_x%d1" % c)
 
@@ -107,14 +113,34 @@ def tile_switchnet_fstar_pa_kernel(tc, x, k1, b1, grad_out, out):
             regroup_gy(unit, c, rh, j, R_HALF // 2 if shared else R_HALF)
             return hand_over(unit)
 
-        def regroup_gy(unit, c, rh, j, vector_share):
-            src = raw_g[c, rh][:].rearrange("p t (r j m) -> p j r t m", j=BLOCKS, m=M)
+        def regroup_rows(unit, c, rh, j, first, end, copy):
+            loads = raw_g[c, rh]
+            per_load = R_HALF // len(loads)
+            start = first // per_load * per_load
+            src = loads[first // per_load][:].rearrange("p t (r j m) -> p j r t m", j=BLOCKS, m=M)
             dst = unit[0][:].rearrange("p (r m t) -> p r t m", m=M, t=PACK)
-            nc.vector.tensor_copy(out=dst[:, 0:vector_share], in_=src[:, j, 0:vector_share])
+            copy(out=dst[:, first:end], in_=src[:, j, first - start : end - start])
+
+        def regroup_gy(unit, c, rh, j, vector_share):
+            regroup_rows(unit, c, rh, j, 0, vector_share, nc.vector.tensor_copy)
             if vector_share < R_HALF:
-                nc.scalar.copy(
-                    out=dst[:, vector_share:R_HALF], in_=src[:, j, vector_share:R_HALF]
+                regroup_rows(unit, c, rh, j, vector_share, R_HALF, nc.scalar.copy)
+
+        def prepare_piece(c, rh):
+            half = R_HALF // 2
+            units = [new_unit(E5M2X4, "g%d%d%d" % (c, rh, j)) for j in range(BLOCKS)]
+            for j in range(BLOCKS):
+                regroup_rows(
+                    units[j], c, rh, j, 0, half, nc.scalar.copy if j % 2 else nc.vector.tensor_copy
                 )
+                if j % 2 and copied:
+                    quantise_copied()
+            for j in (1, 0, 3, 2):
+                regroup_rows(
+                    units[j], c, rh, j, half, R_HALF, nc.vector.tensor_copy if j % 2 else nc.scalar.copy
+                )
+            for j in (1, 0, 3, 2):
+                g_mx[c, rh, j] = hand_over(units[j])
 
         h_mx = {}
         g_mx = {}
@@ -160,6 +186,8 @@ def tile_switchnet_fstar_pa_kernel(tc, x, k1, b1, grad_out, out):
                     regroup_gy(urgent, c, rh, 0, URGENT_VECTOR_SHARE)
                     quantise(urgent)
                     g_mx[c, rh, 0] = urgent[1], urgent[2]
+                elif (c, rh) in IN_TWO_LOADS:
+                    prepare_piece(c, rh)
                 else:
                     for j in range(BLOCKS):
                         g_mx[c, rh, j] = prepare_gy(c, rh, j, True)

@@ -18,8 +18,8 @@ HALVES = 2
 
 X_HALF = 1024
 G_HALF = 2048
-RUN = 8
-RUNS = 4
+WINDOW_ROWS = 16
+X_RUN = 4
 R_HALF = 64
 M = 8
 N_TILE = R_HALF * M
@@ -27,10 +27,8 @@ K_TILE = 128
 K_TILES = 4
 UNIT = N_TILE * PACK
 
-HELD_BACK = (0, 1)
-RUNS_AHEAD = (1, 0)
-IN_TWO_LOADS = ((0, 0), (0, 1), (1, 0))
-URGENT_VECTOR_SHARE = 40
+DMA_ALIGN = 256
+LAST_PIECE = (PASSES - 1, HALVES - 1)
 
 FLOPS = 2 * 4 * 512 * 1024 * 1024
 BYTES = 2 * 1024 * 2048 + 2 * 1024 * 4096 + 4 * 4 * 512 * 1024
@@ -49,39 +47,33 @@ def tile_switchnet_fstar_pa_kernel(tc, x, k1, b1, grad_out, out):
         results = ctx.enter_context(tc.tile_pool(name="results", bufs=6))
         psum = ctx.enter_context(tc.psum_pool(name="psum", bufs=1))
 
-        def load_rows(rows, c, first, width, name):
-            raw = raw_pool.tile([P, PACK, width], BF16, align_bytes=256, name=name)
-            nc.sync.dma_start(
-                out=raw[:],
-                in_=rows[c * K_PASS : (c + 1) * K_PASS, first : first + width].rearrange(
-                    "(p t) f -> p t f", t=PACK
-                ),
-            )
-            return raw
+        def load_rows(rows, c, first, width, loads, name):
+            tiles = []
+            for a in range(loads):
+                raw = raw_pool.tile(
+                    [P, PACK, width // loads], BF16, align_bytes=DMA_ALIGN, name="%s%d" % (name, a)
+                )
+                start = first + a * (width // loads)
+                nc.sync.dma_start(
+                    out=raw[:],
+                    in_=rows[c * K_PASS : (c + 1) * K_PASS, start : start + width // loads].rearrange(
+                        "(p t) f -> p t f", t=PACK
+                    ),
+                )
+                tiles.append(raw)
+            return tiles
 
         raw_x = {}
         raw_g = {}
         for c in range(PASSES):
-            raw_x[c, 0] = load_rows(x_rows, c, 0, X_HALF, "raw_x%d0" % c)
+            raw_x[c, 0] = load_rows(x_rows, c, 0, X_HALF, HALVES, "raw_x%d0" % c)
         for c in range(PASSES):
             for rh in range(HALVES):
-                loads = HALVES if (c, rh) in IN_TWO_LOADS else 1
-                width = G_HALF // loads
-                raw_g[c, rh] = [
-                    load_rows(g_rows, c, rh * G_HALF + a * width, width, "raw_g%d%d%d" % (c, rh, a))
-                    for a in range(loads)
-                ]
+                raw_g[c, rh] = load_rows(g_rows, c, rh * G_HALF, G_HALF, HALVES, "raw_g%d%d" % (c, rh))
         for c in range(PASSES):
-            raw_x[c, 1] = load_rows(x_rows, c, X_HALF, X_HALF, "raw_x%d1" % c)
+            raw_x[c, 1] = load_rows(x_rows, c, X_HALF, X_HALF, 1, "raw_x%d1" % c)
 
-        copied = []
-
-        def quantise(unit):
-            grouped, codes, scales, fp8x4 = unit
-            nc.vector.quantize_mx(out=codes[:].bitcast(fp8x4), scales=scales[:], in_=grouped[:])
-
-        def quantise_copied():
-            quantise(copied.pop())
+        waiting = []
 
         def new_unit(fp8x4, name):
             grouped = stage.tile([P, UNIT], BF16, align_bytes=64, name="grouped")
@@ -89,58 +81,45 @@ def tile_switchnet_fstar_pa_kernel(tc, x, k1, b1, grad_out, out):
             scales = keep.tile([P, N_TILE], U8, align_bytes=64, name="scales_" + name)
             return grouped, codes, scales, fp8x4
 
-        def hand_over(unit):
-            if copied:
-                quantise_copied()
-            copied.append(unit)
-            return unit[1], unit[2]
-
-        def prepare_h(c, j, shared):
-            unit = new_unit(E4M3X4, "h%d%d" % (c, j))
-            src = raw_x[c, j // 2][:].rearrange(
-                "p t (w b g i) -> p b g w t i", b=HALVES, g=RUNS, i=RUN
+        def quantise(unit, first=0, end=N_TILE):
+            grouped, codes, scales, fp8x4 = unit
+            nc.vector.quantize_mx(
+                out=codes[:, first:end].bitcast(fp8x4),
+                scales=scales[:, first:end],
+                in_=grouped[:, first * PACK : end * PACK],
             )
-            dst = unit[0][:].rearrange("p (w g i t) -> p g w t i", g=RUNS, i=RUN, t=PACK)
-            for g in range(RUNS):
-                if shared and g >= RUNS // 2:
-                    nc.scalar.copy(out=dst[:, g], in_=src[:, j % 2, g])
-                else:
-                    nc.vector.tensor_copy(out=dst[:, g], in_=src[:, j % 2, g])
-            return hand_over(unit)
 
-        def prepare_gy(c, rh, j, shared):
-            unit = new_unit(E5M2X4, "g%d%d%d" % (c, rh, j))
-            regroup_gy(unit, c, rh, j, R_HALF // 2 if shared else R_HALF)
-            return hand_over(unit)
+        def quantise_waiting(count):
+            for unused in range(min(count, len(waiting))):
+                quantise(waiting.pop(0))
 
-        def regroup_rows(unit, c, rh, j, first, end, copy):
-            loads = raw_g[c, rh]
-            per_load = R_HALF // len(loads)
-            start = first // per_load * per_load
-            src = loads[first // per_load][:].rearrange("p t (r j m) -> p j r t m", j=BLOCKS, m=M)
-            dst = unit[0][:].rearrange("p (r m t) -> p r t m", m=M, t=PACK)
-            copy(out=dst[:, first:end], in_=src[:, j, first - start : end - start])
+        def regroup(views, first, end, copy):
+            dst, sources = views
+            per_load = dst.shape[1] // len(sources)
+            for a in range(len(sources)):
+                low = max(first, a * per_load)
+                high = min(end, (a + 1) * per_load)
+                if low < high:
+                    copy(out=dst[:, low:high], in_=sources[a][:, low - a * per_load : high - a * per_load])
 
-        def regroup_gy(unit, c, rh, j, vector_share):
-            regroup_rows(unit, c, rh, j, 0, vector_share, nc.vector.tensor_copy)
-            if vector_share < R_HALF:
-                regroup_rows(unit, c, rh, j, vector_share, R_HALF, nc.scalar.copy)
+        def h_views(unit, c, j):
+            runs = K_TILES * K_TILE // WINDOW_ROWS // X_RUN
+            return (
+                unit[0][:].rearrange("p (w g i t) -> p w g t i", g=runs, i=X_RUN, t=PACK),
+                [
+                    raw[:].rearrange("p t (w b g i) -> p b w g t i", b=HALVES, g=runs, i=X_RUN)[:, j % 2]
+                    for raw in raw_x[c, j // 2]
+                ],
+            )
 
-        def prepare_piece(c, rh):
-            half = R_HALF // 2
-            units = [new_unit(E5M2X4, "g%d%d%d" % (c, rh, j)) for j in range(BLOCKS)]
-            for j in range(BLOCKS):
-                regroup_rows(
-                    units[j], c, rh, j, 0, half, nc.scalar.copy if j % 2 else nc.vector.tensor_copy
-                )
-                if j % 2 and copied:
-                    quantise_copied()
-            for j in (1, 0, 3, 2):
-                regroup_rows(
-                    units[j], c, rh, j, half, R_HALF, nc.vector.tensor_copy if j % 2 else nc.scalar.copy
-                )
-            for j in (1, 0, 3, 2):
-                g_mx[c, rh, j] = hand_over(units[j])
+        def g_views(unit, c, rh, j):
+            return (
+                unit[0][:].rearrange("p (r m t) -> p r t m", m=M, t=PACK),
+                [
+                    raw[:].rearrange("p t (r j m) -> p j r t m", j=BLOCKS, m=M)[:, j]
+                    for raw in raw_g[c, rh]
+                ],
+            )
 
         h_mx = {}
         g_mx = {}
@@ -163,7 +142,9 @@ def tile_switchnet_fstar_pa_kernel(tc, x, k1, b1, grad_out, out):
             )
 
         def store_tile(j, kt, copy_first_bank):
-            rows_out = results.tile([P, M, HALVES, R_HALF], F32, align_bytes=256, name="rows_out")
+            rows_out = results.tile(
+                [P, M, HALVES, R_HALF], F32, align_bytes=DMA_ALIGN, name="rows_out"
+            )
             copy_first_bank(
                 out=rows_out[:, :, 0, :], in_=acc[j, kt, 0][:].rearrange("p (r m) -> p m r", m=M)
             )
@@ -175,38 +156,69 @@ def tile_switchnet_fstar_pa_kernel(tc, x, k1, b1, grad_out, out):
                 in_=rows_out[:].rearrange("p m h r -> p (m h r)"),
             )
 
-        last_piece = (PASSES - 1, HALVES - 1)
+        def share_out(views, rows):
+            for a in range(HALVES):
+                for n in range(len(views)):
+                    turn = n if a == 0 else n + 1 - 2 * (n % 2)
+                    by_vector = turn % 2 == a
+                    regroup(
+                        views[turn],
+                        a * rows // 2,
+                        (a + 1) * rows // 2,
+                        nc.vector.tensor_copy if by_vector else nc.scalar.copy,
+                    )
+                    if by_vector and a == 0:
+                        quantise_waiting(1)
+
         for c in range(PASSES):
-            for j in range(HALVES):
-                h_mx[c, j] = prepare_h(c, j, True)
-        for c in range(PASSES):
-            for rh in range(HALVES):
-                if (c, rh) == last_piece:
-                    urgent = new_unit(E5M2X4, "g%d%d0" % (c, rh))
-                    regroup_gy(urgent, c, rh, 0, URGENT_VECTOR_SHARE)
-                    quantise(urgent)
-                    g_mx[c, rh, 0] = urgent[1], urgent[2]
-                elif (c, rh) in IN_TWO_LOADS:
-                    prepare_piece(c, rh)
-                else:
-                    for j in range(BLOCKS):
-                        g_mx[c, rh, j] = prepare_gy(c, rh, j, True)
-                if (c, rh) != HELD_BACK:
-                    for kt in range(K_TILES):
-                        multiply(0, kt, rh, c)
-                if (c, rh) == RUNS_AHEAD:
-                    for kt in range(K_TILES):
-                        multiply(0, kt, HELD_BACK[1], HELD_BACK[0])
+            units = [new_unit(E4M3X4, "h%d%d" % (c, j)) for j in range(HALVES)]
+            share_out([h_views(units[j], c, j) for j in range(HALVES)], WINDOW_ROWS)
+            quantise_waiting(1)
+            for j in (1, 0):
+                h_mx[c, j] = units[j][1], units[j][2]
+                waiting.append(units[j])
+        earlier_pieces = [
+            (c, rh) for c in range(PASSES) for rh in range(HALVES) if (c, rh) != LAST_PIECE
+        ]
+        for c, rh in earlier_pieces:
+            units = [new_unit(E5M2X4, "g%d%d%d" % (c, rh, j)) for j in range(BLOCKS)]
+            share_out([g_views(units[j], c, rh, j) for j in range(BLOCKS)], R_HALF)
+            if (c, rh) == earlier_pieces[-1]:
+                urgent = new_unit(E5M2X4, "g%d%d0" % LAST_PIECE)
+                urgent_views = g_views(urgent, LAST_PIECE[0], LAST_PIECE[1], 0)
+                regroup(urgent_views, 0, R_HALF // 2, nc.vector.tensor_copy)
+            for j in range(BLOCKS):
+                g_mx[c, rh, j] = units[j][1], units[j][2]
+            for j in (1, 0):
+                quantise(units[j])
+            for j in (3, 2):
+                waiting.append(units[j])
+            for kt in range(1 if (c, rh) == earlier_pieces[-1] else K_TILES):
+                multiply(0, kt, rh, c)
+
+        quantise(urgent, 0, N_TILE // 2)
+        regroup(urgent_views, R_HALF // 2, R_HALF, nc.vector.tensor_copy)
+        quantise(urgent, N_TILE // 2, N_TILE)
+        g_mx[LAST_PIECE[0], LAST_PIECE[1], 0] = urgent[1], urgent[2]
+        for kt in range(K_TILES):
+            if kt > 0:
+                multiply(0, kt, earlier_pieces[-1][1], earlier_pieces[-1][0])
+            multiply(0, kt, LAST_PIECE[1], LAST_PIECE[0])
         store_tile(0, 0, nc.scalar.copy)
 
         for j in range(1, BLOCKS):
             if j >= HALVES:
                 for c in range(PASSES):
-                    h_mx[c, j] = prepare_h(c, j, False)
-            g_mx[last_piece[0], last_piece[1], j] = prepare_gy(
-                last_piece[0], last_piece[1], j, False
-            )
-            quantise_copied()
+                    unit = new_unit(E4M3X4, "h%d%d" % (c, j))
+                    regroup(h_views(unit, c, j), 0, WINDOW_ROWS, nc.vector.tensor_copy)
+                    quantise_waiting(1)
+                    waiting.append(unit)
+                    h_mx[c, j] = unit[1], unit[2]
+            unit = new_unit(E5M2X4, "g%d%d%d" % (LAST_PIECE[0], LAST_PIECE[1], j))
+            regroup(g_views(unit, LAST_PIECE[0], LAST_PIECE[1], j), 0, R_HALF, nc.vector.tensor_copy)
+            waiting.append(unit)
+            g_mx[LAST_PIECE[0], LAST_PIECE[1], j] = unit[1], unit[2]
+            quantise_waiting(len(waiting))
             for kt in range(K_TILES):
                 if (j - 1, kt) != (0, 0):
                     store_tile(j - 1, kt, nc.scalar.copy)

@@ -196,6 +196,12 @@ def tile_switchnet_fstar_pa_kernel(tc, x, k1, b1, grad_out, out):
             for kt in range(1 if (c, rh) == earlier_pieces[-1] else K_TILES):
                 multiply(0, kt, rh, c)
 
+        begun = {}
+        for j in (1, 2):
+            unit = new_unit(E5M2X4, "g%d%d%d" % (LAST_PIECE[0], LAST_PIECE[1], j))
+            begun[j] = unit, g_views(unit, LAST_PIECE[0], LAST_PIECE[1], j)
+            regroup(begun[j][1], 0, R_HALF // 2, nc.scalar.copy)
+
         quantise(urgent, 0, N_TILE // 2)
         regroup(urgent_views, R_HALF // 2, R_HALF, nc.vector.tensor_copy)
         quantise(urgent, N_TILE // 2, N_TILE)
@@ -214,8 +220,14 @@ def tile_switchnet_fstar_pa_kernel(tc, x, k1, b1, grad_out, out):
                     quantise_waiting(1)
                     waiting.append(unit)
                     h_mx[c, j] = unit[1], unit[2]
-            unit = new_unit(E5M2X4, "g%d%d%d" % (LAST_PIECE[0], LAST_PIECE[1], j))
-            regroup(g_views(unit, LAST_PIECE[0], LAST_PIECE[1], j), 0, R_HALF, nc.vector.tensor_copy)
+            if j in begun:
+                unit = begun[j][0]
+                regroup(begun[j][1], R_HALF // 2, R_HALF, nc.vector.tensor_copy)
+            else:
+                unit = new_unit(E5M2X4, "g%d%d%d" % (LAST_PIECE[0], LAST_PIECE[1], j))
+                regroup(
+                    g_views(unit, LAST_PIECE[0], LAST_PIECE[1], j), 0, R_HALF, nc.vector.tensor_copy
+                )
             waiting.append(unit)
             g_mx[LAST_PIECE[0], LAST_PIECE[1], j] = unit[1], unit[2]
             quantise_waiting(len(waiting))

@@ -1,6 +1,7 @@
 from contextlib import ExitStack
 
 import concourse.mybir as mybir
+from concourse.masks import make_identity
 
 BF16 = mybir.dt.bfloat16
 F32 = mybir.dt.float32
@@ -26,6 +27,7 @@ N_TILE = R_HALF * M
 K_TILE = 128
 K_TILES = 4
 UNIT = N_TILE * PACK
+BANKS = K_TILES * HALVES
 
 DMA_ALIGN = 256
 LAST_PIECE = (PASSES - 1, HALVES - 1)
@@ -42,44 +44,61 @@ def tile_switchnet_fstar_pa_kernel(tc, x, k1, b1, grad_out, out):
     with ExitStack() as ctx:
         ctx.enter_context(tc.manual_schedule())
         raw_pool = ctx.enter_context(tc.tile_pool(name="raw", bufs=1))
-        stage = ctx.enter_context(tc.tile_pool(name="stage", bufs=8))
+        stage = ctx.enter_context(tc.tile_pool(name="stage", bufs=12))
         keep = ctx.enter_context(tc.tile_pool(name="keep", bufs=1))
         results = ctx.enter_context(tc.tile_pool(name="results", bufs=6))
         psum = ctx.enter_context(tc.psum_pool(name="psum", bufs=1))
 
-        def load_rows(rows, c, first, width, loads, name):
-            tiles = []
-            for a in range(loads):
-                raw = raw_pool.tile(
-                    [P, PACK, width // loads], BF16, align_bytes=DMA_ALIGN, name="%s%d" % (name, a)
-                )
-                start = first + a * (width // loads)
-                nc.sync.dma_start(
-                    out=raw[:],
-                    in_=rows[c * K_PASS : (c + 1) * K_PASS, start : start + width // loads].rearrange(
-                        "(p t) f -> p t f", t=PACK
-                    ),
-                )
-                tiles.append(raw)
-            return tiles
+        def load_rows(rows, c, first, width, name):
+            raw = raw_pool.tile([P, PACK, width], BF16, align_bytes=DMA_ALIGN, name=name)
+            nc.sync.dma_start(
+                out=raw[:],
+                in_=rows[c * K_PASS : (c + 1) * K_PASS, first : first + width].rearrange(
+                    "(p t) f -> p t f", t=PACK
+                ),
+            )
+            return raw
 
         raw_x = {}
         raw_g = {}
         for c in range(PASSES):
-            raw_x[c, 0] = load_rows(x_rows, c, 0, X_HALF, HALVES, "raw_x%d0" % c)
-        for c in range(PASSES):
             for rh in range(HALVES):
-                raw_g[c, rh] = load_rows(g_rows, c, rh * G_HALF, G_HALF, HALVES, "raw_g%d%d" % (c, rh))
+                raw_g[c, rh] = [
+                    load_rows(g_rows, c, rh * G_HALF + a * G_HALF // 2, G_HALF // 2, "raw_g%d%d%d" % (c, rh, a))
+                    for a in range(HALVES)
+                ]
         for c in range(PASSES):
-            raw_x[c, 1] = load_rows(x_rows, c, X_HALF, X_HALF, 1, "raw_x%d1" % c)
+            raw_x[c, 0] = []
+        for a in range(HALVES):
+            for c in range(PASSES):
+                raw_x[c, 0].append(
+                    load_rows(x_rows, c, a * X_HALF // 2, X_HALF // 2, "raw_x%d0%d" % (c, a))
+                )
+        for c in range(PASSES):
+            raw_x[c, 1] = [load_rows(x_rows, c, X_HALF, X_HALF, "raw_x%d1" % c)]
+
+        identity = keep.tile([P, P], BF16, align_bytes=64, name="identity")
+        make_identity(nc, identity[:])
 
         waiting = []
+        h_mx = {}
+        g_mx = {}
 
         def new_unit(fp8x4, name):
             grouped = stage.tile([P, UNIT], BF16, align_bytes=64, name="grouped")
             codes = keep.tile([P, N_TILE], U32, align_bytes=64, name="codes_" + name)
             scales = keep.tile([P, N_TILE], U8, align_bytes=64, name="scales_" + name)
             return grouped, codes, scales, fp8x4
+
+        def h_unit(c, j):
+            unit = new_unit(E4M3X4, "h%d%d" % (c, j))
+            h_mx[c, j] = unit[1], unit[2]
+            return unit
+
+        def g_unit(c, rh, j):
+            unit = new_unit(E5M2X4, "g%d%d%d" % (c, rh, j))
+            g_mx[c, rh, j] = unit[1], unit[2]
+            return unit
 
         def quantise(unit, first=0, end=N_TILE):
             grouped, codes, scales, fp8x4 = unit
@@ -89,57 +108,95 @@ def tile_switchnet_fstar_pa_kernel(tc, x, k1, b1, grad_out, out):
                 in_=grouped[:, first * PACK : end * PACK],
             )
 
-        def quantise_waiting(count):
-            for unused in range(min(count, len(waiting))):
+        def quantise_waiting():
+            if waiting:
                 quantise(waiting.pop(0))
 
-        def regroup(views, first, end, copy):
-            dst, sources = views
-            per_load = dst.shape[1] // len(sources)
-            for a in range(len(sources)):
-                low = max(first, a * per_load)
-                high = min(end, (a + 1) * per_load)
-                if low < high:
-                    copy(out=dst[:, low:high], in_=sources[a][:, low - a * per_load : high - a * per_load])
-
-        def h_views(unit, c, j):
+        def regroup_h(unit, c, j, halves, copy):
             runs = K_TILES * K_TILE // WINDOW_ROWS // X_RUN
-            return (
-                unit[0][:].rearrange("p (w g i t) -> p w g t i", g=runs, i=X_RUN, t=PACK),
-                [
-                    raw[:].rearrange("p t (w b g i) -> p b w g t i", b=HALVES, g=runs, i=X_RUN)[:, j % 2]
-                    for raw in raw_x[c, j // 2]
+            sources = raw_x[c, j // 2]
+            rows = WINDOW_ROWS // HALVES
+            for a in halves:
+                raw = sources[a % len(sources)]
+                view = raw[:].rearrange("p t (w b g i) -> p b w g t i", b=HALVES, g=runs, i=X_RUN)[:, j % 2]
+                low = a * rows if len(sources) == 1 else 0
+                copy(
+                    out=unit[0][:].rearrange("p (w g i t) -> p w g t i", g=runs, i=X_RUN, t=PACK)[
+                        :, a * rows : (a + 1) * rows
+                    ],
+                    in_=view[:, low : low + rows],
+                )
+
+        def regroup_whole_h(unit, c, j, copy):
+            runs = K_TILES * K_TILE // WINDOW_ROWS // X_RUN
+            copy(
+                out=unit[0][:].rearrange("p (w g i t) -> p w g t i", g=runs, i=X_RUN, t=PACK),
+                in_=raw_x[c, j // 2][0][:].rearrange("p t (w b g i) -> p b w g t i", b=HALVES, g=runs, i=X_RUN)[
+                    :, j % 2
                 ],
             )
 
-        def g_views(unit, c, rh, j):
-            return (
-                unit[0][:].rearrange("p (r m t) -> p r t m", m=M, t=PACK),
-                [
-                    raw[:].rearrange("p t (r j m) -> p j r t m", j=BLOCKS, m=M)[:, j]
-                    for raw in raw_g[c, rh]
-                ],
+        def regroup_g(unit, c, rh, j, a, copy):
+            half = R_HALF // HALVES
+            copy(
+                out=unit[0][:].rearrange("p (r m t) -> p r t m", m=M, t=PACK)[:, a * half : (a + 1) * half],
+                in_=raw_g[c, rh][a][:].rearrange("p t (r j m) -> p j r t m", j=BLOCKS, m=M)[:, j],
             )
 
-        h_mx = {}
-        g_mx = {}
+        fills = []
+
+        def fill_bank(view, sizes, source):
+            n = len(fills) % BANKS
+            bank = psum.tile([P, UNIT // HALVES], BF16, name="acc%d%d" % (n // HALVES, n % HALVES))
+            fills.append(bank)
+            dst = bank[:].rearrange(view, **sizes)
+            for t in range(0, PACK, 2):
+                nc.tensor.matmul(
+                    out=dst[:, t : t + 2],
+                    lhsT=identity[:],
+                    rhs=source[:, t : t + 2],
+                    start=True,
+                    stop=True,
+                )
+            return bank
+
+        def fill_g(c, rh, j, a):
+            return fill_bank(
+                "p (r m t) -> p t r m",
+                {"m": M, "t": PACK},
+                raw_g[c, rh][a][:].rearrange("p t (r j m) -> p j t r m", j=BLOCKS, m=M)[:, j],
+            )
+
+        def fill_h(c, j, a):
+            run = K_TILES * K_TILE // WINDOW_ROWS
+            return fill_bank(
+                "p (w e t) -> p t w e",
+                {"e": run, "t": PACK},
+                raw_x[c, j // 2][a][:].rearrange("p t (w b e) -> p b t w e", b=HALVES, e=run)[:, j % 2],
+            )
+
+        def empty_bank(bank, unit, a):
+            half = UNIT // HALVES
+            nc.scalar.copy(out=unit[0][:, a * half : (a + 1) * half].bitcast(F32), in_=bank[:].bitcast(F32))
+
         acc = {}
 
-        def multiply(j, kt, rh, c):
-            if c == 0:
-                acc[j, kt, rh] = psum.tile([P, N_TILE], F32, name="acc%d%d" % (kt, rh))
-            h_codes, h_scales = h_mx[c, j]
-            g_codes, g_scales = g_mx[c, rh, j]
+        def multiply(j, kt):
             k_cols = slice(kt * K_TILE, (kt + 1) * K_TILE)
-            nc.tensor.matmul_mx(
-                out=acc[j, kt, rh][:],
-                lhsT=h_codes[:, k_cols].bitcast(E4M3X4),
-                lhsT_scale=h_scales[:, k_cols],
-                rhs=g_codes[:].bitcast(E5M2X4),
-                rhs_scale=g_scales[:],
-                start=(c == 0),
-                stop=(c == PASSES - 1),
-            )
+            for rh in range(HALVES):
+                acc[j, kt, rh] = psum.tile([P, N_TILE], F32, name="acc%d%d" % (kt, rh))
+                for c in range(PASSES):
+                    h_codes, h_scales = h_mx[c, j]
+                    g_codes, g_scales = g_mx[c, rh, j]
+                    nc.tensor.matmul_mx(
+                        out=acc[j, kt, rh][:],
+                        lhsT=h_codes[:, k_cols].bitcast(E4M3X4),
+                        lhsT_scale=h_scales[:, k_cols],
+                        rhs=g_codes[:].bitcast(E5M2X4),
+                        rhs_scale=g_scales[:],
+                        start=(c == 0),
+                        stop=(c == PASSES - 1),
+                    )
 
         def store_tile(j, kt, copy_first_bank):
             rows_out = results.tile(
@@ -156,86 +213,68 @@ def tile_switchnet_fstar_pa_kernel(tc, x, k1, b1, grad_out, out):
                 in_=rows_out[:].rearrange("p m h r -> p (m h r)"),
             )
 
-        def share_out(views, rows):
-            for a in range(HALVES):
-                for n in range(len(views)):
-                    turn = n if a == 0 else n + 1 - 2 * (n % 2)
-                    by_vector = turn % 2 == a
-                    regroup(
-                        views[turn],
-                        a * rows // 2,
-                        (a + 1) * rows // 2,
-                        nc.vector.tensor_copy if by_vector else nc.scalar.copy,
-                    )
-                    if by_vector and a == 0:
-                        quantise_waiting(1)
+        by_vector = nc.vector.tensor_copy
+        by_scalar = nc.scalar.copy
 
         for c in range(PASSES):
-            units = [new_unit(E4M3X4, "h%d%d" % (c, j)) for j in range(HALVES)]
-            share_out([h_views(units[j], c, j) for j in range(HALVES)], WINDOW_ROWS)
-            quantise_waiting(1)
-            for j in (1, 0):
-                h_mx[c, j] = units[j][1], units[j][2]
-                waiting.append(units[j])
-        earlier_pieces = [
-            (c, rh) for c in range(PASSES) for rh in range(HALVES) if (c, rh) != LAST_PIECE
-        ]
-        for c, rh in earlier_pieces:
-            units = [new_unit(E5M2X4, "g%d%d%d" % (c, rh, j)) for j in range(BLOCKS)]
-            share_out([g_views(units[j], c, rh, j) for j in range(BLOCKS)], R_HALF)
-            if (c, rh) == earlier_pieces[-1]:
-                urgent = new_unit(E5M2X4, "g%d%d0" % LAST_PIECE)
-                urgent_views = g_views(urgent, LAST_PIECE[0], LAST_PIECE[1], 0)
-                regroup(urgent_views, 0, R_HALF // 2, nc.vector.tensor_copy)
-            for j in range(BLOCKS):
-                g_mx[c, rh, j] = units[j][1], units[j][2]
-            for j in (1, 0):
-                quantise(units[j])
-            for j in (3, 2):
-                waiting.append(units[j])
-            for kt in range(1 if (c, rh) == earlier_pieces[-1] else K_TILES):
-                multiply(0, kt, rh, c)
+            for rh in range(HALVES):
+                units = [g_unit(c, rh, j) for j in range(BLOCKS)]
+                bank3 = fill_g(c, rh, 3, 0)
+                bank2 = fill_g(c, rh, 2, 0) if c == 0 else None
+                regroup_g(units[0], c, rh, 0, 0, by_vector)
+                quantise_waiting()
+                regroup_g(units[1], c, rh, 1, 0, by_scalar)
+                quantise_waiting()
+                empty_bank(bank3, units[3], 0)
+                if c == 0:
+                    empty_bank(bank2, units[2], 0)
+                else:
+                    regroup_g(units[2], c, rh, 2, 0, by_scalar)
+                bank3 = fill_g(c, rh, 3, 1)
+                regroup_g(units[0], c, rh, 0, 1, by_vector)
+                regroup_g(units[1], c, rh, 1, 1, by_vector)
+                regroup_g(units[2], c, rh, 2, 1, by_scalar)
+                empty_bank(bank3, units[3], 1)
+                quantise(units[0])
+                if (c, rh) == LAST_PIECE:
+                    waiting.append(units[1])
+                else:
+                    quantise(units[1])
+                waiting.append(units[2])
+                waiting.append(units[3])
 
-        begun = {}
-        for j in (1, 2):
-            unit = new_unit(E5M2X4, "g%d%d%d" % (LAST_PIECE[0], LAST_PIECE[1], j))
-            begun[j] = unit, g_views(unit, LAST_PIECE[0], LAST_PIECE[1], j)
-            regroup(begun[j][1], 0, R_HALF // 2, nc.scalar.copy)
-
-        quantise(urgent, 0, N_TILE // 2)
-        regroup(urgent_views, R_HALF // 2, R_HALF, nc.vector.tensor_copy)
-        quantise(urgent, N_TILE // 2, N_TILE)
-        g_mx[LAST_PIECE[0], LAST_PIECE[1], 0] = urgent[1], urgent[2]
-        for kt in range(K_TILES):
-            if kt > 0:
-                multiply(0, kt, earlier_pieces[-1][1], earlier_pieces[-1][0])
-            multiply(0, kt, LAST_PIECE[1], LAST_PIECE[0])
-        store_tile(0, 0, nc.scalar.copy)
+        units = {}
+        for j in range(HALVES):
+            for c in range(PASSES):
+                units[c, j] = h_unit(c, j)
+        banks = [fill_h(c, 1, 0) for c in range(PASSES)]
+        for c in range(PASSES):
+            empty_bank(banks[c], units[c, 1], 0)
+        for a in range(HALVES):
+            for c in range(PASSES):
+                regroup_h(units[c, 0], c, 0, [a], by_vector)
+            for c in range(PASSES):
+                quantise(units[c, 0], a * N_TILE // HALVES, (a + 1) * N_TILE // HALVES)
+            for kt in range(a * K_TILES // HALVES, (a + 1) * K_TILES // HALVES):
+                multiply(0, kt)
+            if a == 0:
+                quantise_waiting()
+        store_tile(0, 0, by_scalar)
 
         for j in range(1, BLOCKS):
-            if j >= HALVES:
-                for c in range(PASSES):
-                    unit = new_unit(E4M3X4, "h%d%d" % (c, j))
-                    regroup(h_views(unit, c, j), 0, WINDOW_ROWS, nc.vector.tensor_copy)
-                    quantise_waiting(1)
-                    waiting.append(unit)
-                    h_mx[c, j] = unit[1], unit[2]
-            if j in begun:
-                unit = begun[j][0]
-                regroup(begun[j][1], R_HALF // 2, R_HALF, nc.vector.tensor_copy)
-            else:
-                unit = new_unit(E5M2X4, "g%d%d%d" % (LAST_PIECE[0], LAST_PIECE[1], j))
-                regroup(
-                    g_views(unit, LAST_PIECE[0], LAST_PIECE[1], j), 0, R_HALF, nc.vector.tensor_copy
-                )
-            waiting.append(unit)
-            g_mx[LAST_PIECE[0], LAST_PIECE[1], j] = unit[1], unit[2]
-            quantise_waiting(len(waiting))
+            for c in range(PASSES):
+                if j == 1:
+                    regroup_h(units[c, j], c, j, [1], by_vector)
+                else:
+                    units[c, j] = h_unit(c, j)
+                    regroup_whole_h(units[c, j], c, j, by_vector)
+                if c == 1:
+                    quantise(units[0, j])
+            quantise_waiting()
+            quantise(units[1, j])
             for kt in range(K_TILES):
                 if (j - 1, kt) != (0, 0):
-                    store_tile(j - 1, kt, nc.scalar.copy)
-                for rh in range(HALVES):
-                    for c in range(PASSES):
-                        multiply(j, kt, rh, c)
+                    store_tile(j - 1, kt, by_scalar)
+                multiply(j, kt)
         for kt in range(K_TILES):
-            store_tile(BLOCKS - 1, kt, nc.vector.tensor_copy)
+            store_tile(BLOCKS - 1, kt, by_vector)

@@ -27,10 +27,10 @@ N_TILE = R_HALF * M
 K_TILE = 128
 K_TILES = 4
 UNIT = N_TILE * PACK
-BANKS = K_TILES * HALVES
+FILL_BANKS = 4
 
 DMA_ALIGN = 256
-LAST_PIECE = (PASSES - 1, HALVES - 1)
+LAST_LOAD = (PASSES - 1, HALVES - 1, HALVES - 1)
 
 FLOPS = 2 * 4 * 512 * 1024 * 1024
 BYTES = 2 * 1024 * 2048 + 2 * 1024 * 4096 + 4 * 4 * 512 * 1024
@@ -61,21 +61,26 @@ def tile_switchnet_fstar_pa_kernel(tc, x, k1, b1, grad_out, out):
 
         raw_x = {}
         raw_g = {}
+
+        def load_x(c, br, a, loads):
+            width = X_HALF // loads
+            raw_x.setdefault((c, br), []).append(
+                load_rows(x_rows, c, br * X_HALF + a * width, width, "raw_x%d%d%d" % (c, br, a))
+            )
+
+        load_x(0, 0, 0, 1)
         for c in range(PASSES):
             for rh in range(HALVES):
-                raw_g[c, rh] = [
-                    load_rows(g_rows, c, rh * G_HALF + a * G_HALF // 2, G_HALF // 2, "raw_g%d%d%d" % (c, rh, a))
-                    for a in range(HALVES)
-                ]
+                for a in range(HALVES):
+                    if (c, rh, a) == LAST_LOAD:
+                        load_x(1, 0, 0, HALVES)
+                    width = G_HALF // HALVES
+                    raw_g.setdefault((c, rh), []).append(
+                        load_rows(g_rows, c, rh * G_HALF + a * width, width, "raw_g%d%d%d" % (c, rh, a))
+                    )
+        load_x(1, 0, 1, HALVES)
         for c in range(PASSES):
-            raw_x[c, 0] = []
-        for a in range(HALVES):
-            for c in range(PASSES):
-                raw_x[c, 0].append(
-                    load_rows(x_rows, c, a * X_HALF // 2, X_HALF // 2, "raw_x%d0%d" % (c, a))
-                )
-        for c in range(PASSES):
-            raw_x[c, 1] = [load_rows(x_rows, c, X_HALF, X_HALF, "raw_x%d1" % c)]
+            load_x(c, 1, 0, 1)
 
         identity = keep.tile([P, P], BF16, align_bytes=64, name="identity")
         make_identity(nc, identity[:])
@@ -112,27 +117,14 @@ def tile_switchnet_fstar_pa_kernel(tc, x, k1, b1, grad_out, out):
             if waiting:
                 quantise(waiting.pop(0))
 
-        def regroup_h(unit, c, j, halves, copy):
+        def regroup_h(unit, c, j, first, end, copy):
             runs = K_TILES * K_TILE // WINDOW_ROWS // X_RUN
-            sources = raw_x[c, j // 2]
-            rows = WINDOW_ROWS // HALVES
-            for a in halves:
-                raw = sources[a % len(sources)]
-                view = raw[:].rearrange("p t (w b g i) -> p b w g t i", b=HALVES, g=runs, i=X_RUN)[:, j % 2]
-                low = a * rows if len(sources) == 1 else 0
-                copy(
-                    out=unit[0][:].rearrange("p (w g i t) -> p w g t i", g=runs, i=X_RUN, t=PACK)[
-                        :, a * rows : (a + 1) * rows
-                    ],
-                    in_=view[:, low : low + rows],
-                )
-
-        def regroup_whole_h(unit, c, j, copy):
-            runs = K_TILES * K_TILE // WINDOW_ROWS // X_RUN
+            loads = raw_x[c, j // 2]
+            a, low = divmod(first, WINDOW_ROWS // len(loads))
             copy(
-                out=unit[0][:].rearrange("p (w g i t) -> p w g t i", g=runs, i=X_RUN, t=PACK),
-                in_=raw_x[c, j // 2][0][:].rearrange("p t (w b g i) -> p b w g t i", b=HALVES, g=runs, i=X_RUN)[
-                    :, j % 2
+                out=unit[0][:].rearrange("p (w g i t) -> p w g t i", g=runs, i=X_RUN, t=PACK)[:, first:end],
+                in_=loads[a][:].rearrange("p t (w b g i) -> p b w g t i", b=HALVES, g=runs, i=X_RUN)[
+                    :, j % 2, low : low + end - first
                 ],
             )
 
@@ -146,8 +138,9 @@ def tile_switchnet_fstar_pa_kernel(tc, x, k1, b1, grad_out, out):
         fills = []
 
         def fill_bank(view, sizes, source):
-            n = len(fills) % BANKS
-            bank = psum.tile([P, UNIT // HALVES], BF16, name="acc%d%d" % (n // HALVES, n % HALVES))
+            kt, rh = divmod(len(fills) % FILL_BANKS, HALVES)
+            kt += K_TILES - FILL_BANKS // HALVES
+            bank = psum.tile([P, UNIT // HALVES], BF16, name="acc%d%d" % (kt, rh))
             fills.append(bank)
             dst = bank[:].rearrange(view, **sizes)
             for t in range(0, PACK, 2):
@@ -181,11 +174,12 @@ def tile_switchnet_fstar_pa_kernel(tc, x, k1, b1, grad_out, out):
 
         acc = {}
 
-        def multiply(j, kt):
+        def multiply(j, kt, passes=range(PASSES), halves=range(HALVES)):
             k_cols = slice(kt * K_TILE, (kt + 1) * K_TILE)
-            for rh in range(HALVES):
-                acc[j, kt, rh] = psum.tile([P, N_TILE], F32, name="acc%d%d" % (kt, rh))
-                for c in range(PASSES):
+            for rh in halves:
+                for c in passes:
+                    if c == 0:
+                        acc[j, kt, rh] = psum.tile([P, N_TILE], F32, name="acc%d%d" % (kt, rh))
                     h_codes, h_scales = h_mx[c, j]
                     g_codes, g_scales = g_mx[c, rh, j]
                     nc.tensor.matmul_mx(
@@ -216,64 +210,84 @@ def tile_switchnet_fstar_pa_kernel(tc, x, k1, b1, grad_out, out):
         by_vector = nc.vector.tensor_copy
         by_scalar = nc.scalar.copy
 
+        half = WINDOW_ROWS // HALVES
+        half_unit = N_TILE // HALVES
+        h = {(0, j): h_unit(0, j) for j in range(HALVES)}
+        regroup_h(h[0, 0], 0, 0, 0, WINDOW_ROWS, by_vector)
+        regroup_h(h[0, 1], 0, 1, 0, WINDOW_ROWS, by_scalar)
+        waiting.extend([h[0, 0], h[0, 1]])
+
         for c in range(PASSES):
             for rh in range(HALVES):
-                units = [g_unit(c, rh, j) for j in range(BLOCKS)]
+                last = (c, rh) == LAST_LOAD[:2]
+                g = [g_unit(c, rh, j) for j in range(BLOCKS)]
                 bank3 = fill_g(c, rh, 3, 0)
-                bank2 = fill_g(c, rh, 2, 0) if c == 0 else None
-                regroup_g(units[0], c, rh, 0, 0, by_vector)
+                bank2 = None if last else fill_g(c, rh, 2, 0)
+                if (c, rh) == (1, 0):
+                    for kt in range(K_TILES - FILL_BANKS // HALVES):
+                        multiply(0, kt, (0,))
+                regroup_g(g[0], c, rh, 0, 0, by_vector)
                 quantise_waiting()
-                regroup_g(units[1], c, rh, 1, 0, by_scalar)
-                quantise_waiting()
-                empty_bank(bank3, units[3], 0)
-                if c == 0:
-                    empty_bank(bank2, units[2], 0)
+                regroup_g(g[1], c, rh, 1, 0, by_scalar)
+                empty_bank(bank3, g[3], 0)
+                if last:
+                    regroup_g(g[2], c, rh, 2, 0, by_scalar)
                 else:
-                    regroup_g(units[2], c, rh, 2, 0, by_scalar)
-                bank3 = fill_g(c, rh, 3, 1)
-                regroup_g(units[0], c, rh, 0, 1, by_vector)
-                regroup_g(units[1], c, rh, 1, 1, by_vector)
-                regroup_g(units[2], c, rh, 2, 1, by_scalar)
-                empty_bank(bank3, units[3], 1)
-                quantise(units[0])
-                if (c, rh) == LAST_PIECE:
-                    waiting.append(units[1])
-                else:
-                    quantise(units[1])
-                waiting.append(units[2])
-                waiting.append(units[3])
+                    quantise_waiting()
+                    empty_bank(bank2, g[2], 0)
+                    bank3 = fill_g(c, rh, 3, 1)
+                    regroup_g(g[0], c, rh, 0, 1, by_vector)
+                    regroup_g(g[1], c, rh, 1, 1, by_vector)
+                    quantise(g[0])
+                    quantise(g[1])
+                    regroup_g(g[2], c, rh, 2, 1, by_scalar)
+                    empty_bank(bank3, g[3], 1)
+                    waiting.extend([g[2], g[3]])
 
-        units = {}
         for j in range(HALVES):
-            for c in range(PASSES):
-                units[c, j] = h_unit(c, j)
-        banks = [fill_h(c, 1, 0) for c in range(PASSES)]
-        for c in range(PASSES):
-            empty_bank(banks[c], units[c, 1], 0)
-        for a in range(HALVES):
-            for c in range(PASSES):
-                regroup_h(units[c, 0], c, 0, [a], by_vector)
-            for c in range(PASSES):
-                quantise(units[c, 0], a * N_TILE // HALVES, (a + 1) * N_TILE // HALVES)
-            for kt in range(a * K_TILES // HALVES, (a + 1) * K_TILES // HALVES):
-                multiply(0, kt)
-            if a == 0:
-                quantise_waiting()
+            h[1, j] = h_unit(1, j)
+        bank = fill_h(1, 1, 0)
+        regroup_h(h[1, 0], 1, 0, 0, half, by_vector)
+        quantise_waiting()
+        quantise(g[0], 0, half_unit)
+        quantise(h[1, 0], 0, half_unit)
+        empty_bank(bank, h[1, 1], 0)
+
+        c, rh, a = LAST_LOAD
+        bank3 = fill_g(c, rh, 3, a)
+        regroup_g(g[0], c, rh, 0, a, by_vector)
+        quantise(g[0], half_unit, N_TILE)
+        multiply(0, 0, (1,), (0,))
+        empty_bank(bank3, g[3], a)
+        multiply(0, 2, (0,))
+        multiply(0, 0, (1,), (1,))
+        multiply(0, 1, (1,))
         store_tile(0, 0, by_scalar)
+        multiply(0, 3, (0,))
+
+        regroup_h(h[1, 0], 1, 0, half, WINDOW_ROWS, by_vector)
+        regroup_h(h[1, 1], 1, 1, half, WINDOW_ROWS, by_vector)
+        quantise(h[1, 0], half_unit, N_TILE)
+        multiply(0, 2, (1,))
+        store_tile(0, 1, by_scalar)
+        multiply(0, 3, (1,))
+        regroup_g(g[1], c, rh, 1, a, by_vector)
+        quantise(h[1, 1])
+        quantise(g[1])
+        regroup_g(g[2], c, rh, 2, a, by_vector)
+        waiting.extend([g[2], g[3]])
 
         for j in range(1, BLOCKS):
-            for c in range(PASSES):
-                if j == 1:
-                    regroup_h(units[c, j], c, j, [1], by_vector)
-                else:
-                    units[c, j] = h_unit(c, j)
-                    regroup_whole_h(units[c, j], c, j, by_vector)
-                if c == 1:
-                    quantise(units[0, j])
-            quantise_waiting()
-            quantise(units[1, j])
+            if j >= HALVES:
+                for c in range(PASSES):
+                    h[c, j] = h_unit(c, j)
+                    regroup_h(h[c, j], c, j, 0, WINDOW_ROWS, by_vector)
+                    if c == 1:
+                        quantise(h[0, j])
+                quantise(h[1, j])
+                quantise_waiting()
             for kt in range(K_TILES):
-                if (j - 1, kt) != (0, 0):
+                if (j - 1, kt) not in ((0, 0), (0, 1)):
                     store_tile(j - 1, kt, by_scalar)
                 multiply(j, kt)
         for kt in range(K_TILES):

@@ -21,6 +21,7 @@ X_HALF = 1024
 G_HALF = 2048
 WINDOW_ROWS = 16
 X_RUN = 4
+G_RUN = 4
 R_HALF = 64
 M = 8
 N_TILE = R_HALF * M
@@ -131,8 +132,12 @@ def tile_switchnet_fstar_pa_kernel(tc, x, k1, b1, grad_out, out):
         def regroup_g(unit, c, rh, j, a, copy):
             half = R_HALF // HALVES
             copy(
-                out=unit[0][:].rearrange("p (r m t) -> p r t m", m=M, t=PACK)[:, a * half : (a + 1) * half],
-                in_=raw_g[c, rh][a][:].rearrange("p t (r j m) -> p j r t m", j=BLOCKS, m=M)[:, j],
+                out=unit[0][:].rearrange("p (r n i t) -> p r n t i", n=M // G_RUN, i=G_RUN, t=PACK)[
+                    :, a * half : (a + 1) * half
+                ],
+                in_=raw_g[c, rh][a][:].rearrange("p t (r j n i) -> p j r n t i", j=BLOCKS, n=M // G_RUN, i=G_RUN)[
+                    :, j
+                ],
             )
 
         fills = []

from contextlib import ExitStack

import concourse.mybir as mybir
from concourse.masks import make_identity

BF16 = mybir.dt.bfloat16
F32 = mybir.dt.float32
U32 = mybir.dt.uint32
U8 = mybir.dt.uint8
E4M3X4 = mybir.dt.float8_e4m3fn_x4
E5M2X4 = mybir.dt.float8_e5m2_x4

P = 128
PACK = 4
K_PASS = P * PACK
PASSES = 2
BLOCKS = 4
HALVES = 2

X_HALF = 1024
G_HALF = 2048
WINDOW_ROWS = 16
X_RUN = 4
G_RUN = 4
R_HALF = 64
M = 8
N_TILE = R_HALF * M
K_TILE = 128
K_TILES = 4
UNIT = N_TILE * PACK
FILL_BANKS = 4

DMA_ALIGN = 256
LAST_LOAD = (PASSES - 1, HALVES - 1, HALVES - 1)

FLOPS = 2 * 4 * 512 * 1024 * 1024
BYTES = 2 * 1024 * 2048 + 2 * 1024 * 4096 + 4 * 4 * 512 * 1024


def tile_switchnet_fstar_pa_kernel(tc, x, k1, b1, grad_out, out):
    nc = tc.nc
    x_rows = x.rearrange("b g c -> b (g c)")
    g_rows = grad_out.rearrange("b s r -> b (s r)")

    with ExitStack() as ctx:
        ctx.enter_context(tc.manual_schedule())
        raw_pool = ctx.enter_context(tc.tile_pool(name="raw", bufs=1))
        stage = ctx.enter_context(tc.tile_pool(name="stage", bufs=12))
        keep = ctx.enter_context(tc.tile_pool(name="keep", bufs=1))
        results = ctx.enter_context(tc.tile_pool(name="results", bufs=6))
        psum = ctx.enter_context(tc.psum_pool(name="psum", bufs=1))

        def load_rows(rows, c, first, width, name):
            raw = raw_pool.tile([P, PACK, width], BF16, align_bytes=DMA_ALIGN, name=name)
            nc.sync.dma_start(
                out=raw[:],
                in_=rows[c * K_PASS : (c + 1) * K_PASS, first : first + width].rearrange(
                    "(p t) f -> p t f", t=PACK
                ),
            )
            return raw

        raw_x = {}
        raw_g = {}

        def load_x(c, br, a, loads):
            width = X_HALF // loads
            raw_x.setdefault((c, br), []).append(
                load_rows(x_rows, c, br * X_HALF + a * width, width, "raw_x%d%d%d" % (c, br, a))
            )

        load_x(0, 0, 0, 1)
        for c in range(PASSES):
            for rh in range(HALVES):
                for a in range(HALVES):
                    if (c, rh, a) == LAST_LOAD:
                        load_x(1, 0, 0, HALVES)
                    width = G_HALF // HALVES
                    raw_g.setdefault((c, rh), []).append(
                        load_rows(g_rows, c, rh * G_HALF + a * width, width, "raw_g%d%d%d" % (c, rh, a))
                    )
        load_x(1, 0, 1, HALVES)
        for c in range(PASSES):
            load_x(c, 1, 0, 1)

        identity = keep.tile([P, P], BF16, align_bytes=64, name="identity")
        make_identity(nc, identity[:])

        waiting = []
        h_mx = {}
        g_mx = {}

        def new_unit(fp8x4, name):
            grouped = stage.tile([P, UNIT], BF16, align_bytes=64, name="grouped")
            codes = keep.tile([P, N_TILE], U32, align_bytes=64, name="codes_" + name)
            scales = keep.tile([P, N_TILE], U8, align_bytes=64, name="scales_" + name)
            return grouped, codes, scales, fp8x4

        def h_unit(c, j):
            unit = new_unit(E4M3X4, "h%d%d" % (c, j))
            h_mx[c, j] = unit[1], unit[2]
            return unit

        def g_unit(c, rh, j):
            unit = new_unit(E5M2X4, "g%d%d%d" % (c, rh, j))
            g_mx[c, rh, j] = unit[1], unit[2]
            return unit

        def quantise(unit, first=0, end=N_TILE):
            grouped, codes, scales, fp8x4 = unit
            nc.vector.quantize_mx(
                out=codes[:, first:end].bitcast(fp8x4),
                scales=scales[:, first:end],
                in_=grouped[:, first * PACK : end * PACK],
            )

        def quantise_waiting():
            if waiting:
                quantise(waiting.pop(0))

        def regroup_h(unit, c, j, first, end, copy):
            runs = K_TILES * K_TILE // WINDOW_ROWS // X_RUN
            loads = raw_x[c, j // 2]
            a, low = divmod(first, WINDOW_ROWS // len(loads))
            copy(
                out=unit[0][:].rearrange("p (w g i t) -> p w g t i", g=runs, i=X_RUN, t=PACK)[:, first:end],
                in_=loads[a][:].rearrange("p t (w b g i) -> p b w g t i", b=HALVES, g=runs, i=X_RUN)[
                    :, j % 2, low : low + end - first
                ],
            )

        def regroup_g(unit, c, rh, j, a, copy):
            half = R_HALF // HALVES
            copy(
                out=unit[0][:].rearrange("p (r n i t) -> p r n t i", n=M // G_RUN, i=G_RUN, t=PACK)[
                    :, a * half : (a + 1) * half
                ],
                in_=raw_g[c, rh][a][:].rearrange("p t (r j n i) -> p j r n t i", j=BLOCKS, n=M // G_RUN, i=G_RUN)[
                    :, j
                ],
            )

        fills = []

        def fill_bank(view, sizes, source):
            kt, rh = divmod(len(fills) % FILL_BANKS, HALVES)
            kt += K_TILES - FILL_BANKS // HALVES
            bank = psum.tile([P, UNIT // HALVES], BF16, name="acc%d%d" % (kt, rh))
            fills.append(bank)
            dst = bank[:].rearrange(view, **sizes)
            for t in range(0, PACK, 2):
                nc.tensor.matmul(
                    out=dst[:, t : t + 2],
                    lhsT=identity[:],
                    rhs=source[:, t : t + 2],
                    start=True,
                    stop=True,
                )
            return bank

        def fill_g(c, rh, j, a):
            return fill_bank(
                "p (r m t) -> p t r m",
                {"m": M, "t": PACK},
                raw_g[c, rh][a][:].rearrange("p t (r j m) -> p j t r m", j=BLOCKS, m=M)[:, j],
            )

        def fill_h(c, j, a):
            run = K_TILES * K_TILE // WINDOW_ROWS
            return fill_bank(
                "p (w e t) -> p t w e",
                {"e": run, "t": PACK},
                raw_x[c, j // 2][a][:].rearrange("p t (w b e) -> p b t w e", b=HALVES, e=run)[:, j % 2],
            )

        def empty_bank(bank, unit, a):
            half = UNIT // HALVES
            nc.scalar.copy(out=unit[0][:, a * half : (a + 1) * half].bitcast(F32), in_=bank[:].bitcast(F32))

        acc = {}

        def multiply(j, kt, passes=range(PASSES), halves=range(HALVES)):
            k_cols = slice(kt * K_TILE, (kt + 1) * K_TILE)
            for rh in halves:
                for c in passes:
                    if c == 0:
                        acc[j, kt, rh] = psum.tile([P, N_TILE], F32, name="acc%d%d" % (kt, rh))
                    h_codes, h_scales = h_mx[c, j]
                    g_codes, g_scales = g_mx[c, rh, j]
                    nc.tensor.matmul_mx(
                        out=acc[j, kt, rh][:],
                        lhsT=h_codes[:, k_cols].bitcast(E4M3X4),
                        lhsT_scale=h_scales[:, k_cols],
                        rhs=g_codes[:].bitcast(E5M2X4),
                        rhs_scale=g_scales[:],
                        start=(c == 0),
                        stop=(c == PASSES - 1),
                    )

        def store_tile(j, kt, copy_first_bank):
            rows_out = results.tile(
                [P, M, HALVES, R_HALF], F32, align_bytes=DMA_ALIGN, name="rows_out"
            )
            copy_first_bank(
                out=rows_out[:, :, 0, :], in_=acc[j, kt, 0][:].rearrange("p (r m) -> p m r", m=M)
            )
            nc.scalar.copy(
                out=rows_out[:, :, 1, :], in_=acc[j, kt, 1][:].rearrange("p (r m) -> p m r", m=M)
            )
            nc.sync.dma_start(
                out=out[j, kt * K_TILE : (kt + 1) * K_TILE, :],
                in_=rows_out[:].rearrange("p m h r -> p (m h r)"),
            )

        by_vector = nc.vector.tensor_copy
        by_scalar = nc.scalar.copy

        half = WINDOW_ROWS // HALVES
        half_unit = N_TILE // HALVES
        h = {(0, j): h_unit(0, j) for j in range(HALVES)}
        regroup_h(h[0, 0], 0, 0, 0, WINDOW_ROWS, by_vector)
        regroup_h(h[0, 1], 0, 1, 0, WINDOW_ROWS, by_scalar)
        waiting.extend([h[0, 0], h[0, 1]])

        for c in range(PASSES):
            for rh in range(HALVES):
                last = (c, rh) == LAST_LOAD[:2]
                g = [g_unit(c, rh, j) for j in range(BLOCKS)]
                bank3 = fill_g(c, rh, 3, 0)
                bank2 = None if last else fill_g(c, rh, 2, 0)
                if (c, rh) == (1, 0):
                    for kt in range(K_TILES - FILL_BANKS // HALVES):
                        multiply(0, kt, (0,))
                regroup_g(g[0], c, rh, 0, 0, by_vector)
                quantise_waiting()
                regroup_g(g[1], c, rh, 1, 0, by_scalar)
                empty_bank(bank3, g[3], 0)
                if last:
                    regroup_g(g[2], c, rh, 2, 0, by_scalar)
                else:
                    quantise_waiting()
                    empty_bank(bank2, g[2], 0)
                    bank3 = fill_g(c, rh, 3, 1)
                    regroup_g(g[0], c, rh, 0, 1, by_vector)
                    regroup_g(g[1], c, rh, 1, 1, by_vector)
                    quantise(g[0])
                    quantise(g[1])
                    regroup_g(g[2], c, rh, 2, 1, by_scalar)
                    empty_bank(bank3, g[3], 1)
                    waiting.extend([g[2], g[3]])

        for j in range(HALVES):
            h[1, j] = h_unit(1, j)
        bank = fill_h(1, 1, 0)
        regroup_h(h[1, 0], 1, 0, 0, half, by_vector)
        quantise_waiting()
        quantise(g[0], 0, half_unit)
        quantise(h[1, 0], 0, half_unit)
        empty_bank(bank, h[1, 1], 0)

        c, rh, a = LAST_LOAD
        bank3 = fill_g(c, rh, 3, a)
        regroup_g(g[0], c, rh, 0, a, by_vector)
        quantise(g[0], half_unit, N_TILE)
        multiply(0, 0, (1,), (0,))
        empty_bank(bank3, g[3], a)
        multiply(0, 2, (0,))
        multiply(0, 0, (1,), (1,))
        multiply(0, 1, (1,))
        store_tile(0, 0, by_scalar)
        multiply(0, 3, (0,))

        regroup_h(h[1, 0], 1, 0, half, WINDOW_ROWS, by_vector)
        regroup_h(h[1, 1], 1, 1, half, WINDOW_ROWS, by_vector)
        quantise(h[1, 0], half_unit, N_TILE)
        multiply(0, 2, (1,))
        store_tile(0, 1, by_scalar)
        multiply(0, 3, (1,))
        regroup_g(g[1], c, rh, 1, a, by_vector)
        quantise(h[1, 1])
        quantise(g[1])
        regroup_g(g[2], c, rh, 2, a, by_vector)
        waiting.extend([g[2], g[3]])

        for j in range(1, BLOCKS):
            if j >= HALVES:
                for c in range(PASSES):
                    h[c, j] = h_unit(c, j)
                    regroup_h(h[c, j], c, j, 0, WINDOW_ROWS, by_vector)
                    if c == 1:
                        quantise(h[0, j])
                quantise(h[1, j])
                quantise_waiting()
            for kt in range(K_TILES):
                if (j - 1, kt) not in ((0, 0), (0, 1)):
                    store_tile(j - 1, kt, by_scalar)
                multiply(j, kt)
        for kt in range(K_TILES):
            store_tile(BLOCKS - 1, kt, by_vector)
